import numpy as np
import ml_dtypes


def mxq(x, axis, fmt="e4m3"):
    dtype, down = {"e4m3": (ml_dtypes.float8_e4m3fn, 7), "e5m2": (ml_dtypes.float8_e5m2, 14)}[fmt]
    v = np.moveaxis(np.asarray(x, np.float32).astype(ml_dtypes.bfloat16).astype(np.float64), axis, -1)
    blocks = v.reshape(v.shape[:-1] + (-1, 32))
    amax = np.abs(blocks).max(-1, keepdims=True)
    byte = np.maximum(np.where(amax > 0, np.frexp(amax)[1] - 1 + 127, 0) - down, 1)
    scale = np.exp2(byte - 127.0)
    codes = (blocks / scale).astype(np.float32).astype(dtype).astype(np.float64)
    return np.moveaxis((codes * scale).reshape(v.shape), -1, axis)


WIDE = False


def mx_kscale(k):
    if not WIDE:
        return np.ones(k)
    levels = np.array([10, -10, 5, -5, 0])
    if k % 512:
        return np.exp2(np.random.permutation(np.resize(levels, k // 32))).repeat(32)
    a = np.empty((k // 512, 16))
    for p in range(k // 512):
        a[p, :8] = np.random.permutation(np.resize(levels, 8))
        for g in range(8):
            far = levels[np.abs(levels - a[p, g]) >= 10]
            a[p, g + 8] = far[np.random.randint(len(far))]
    return np.exp2(a.ravel()).repeat(32)


BF16 = ml_dtypes.bfloat16


def bf(x):
    return np.asarray(x, np.float32).astype(BF16)


def f64(x):
    return np.asarray(x).astype(np.float64)


B, N, C, F = 4, 32, 1024, 1024
EPS_STD = 1e-5


def setup_inputs():
    u, s = mx_kscale(C), mx_kscale(C)
    rows = np.concatenate([u, u, s])
    return {"x": bf(np.random.standard_normal((B, N, C)) * u),
            "e_enc": bf(np.random.standard_normal((B, N, N, C)) * s),
            "W_pre": bf(np.random.standard_normal((3 * C, F)) / np.sqrt(3 * C) / rows[:, None]),
            "b_pre": bf(np.random.standard_normal(F) * 0.3)}


def core(x, e_enc, W_pre, b_pre):
    w = f64(W_pre)
    xq = mxq(f64(x), 2, "e4m3")
    tgt = xq @ mxq(w[:C], 0, "e4m3")
    src = xq @ mxq(w[C:2 * C], 0, "e4m3")
    edg = mxq(f64(e_enc), 3, "e4m3") @ mxq(w[2 * C:], 0, "e4m3")
    m = tgt[:, :, None, :] + src[:, None, :, :] + edg + f64(b_pre)
    mean = m.mean(axis=2)
    mn = m.min(axis=2)
    mx = m.max(axis=2)
    var = (m * m).mean(axis=2) - mean * mean
    std = np.sqrt(np.maximum(var, 0.0) + EPS_STD)
    return np.concatenate([mean, mn, mx, std], axis=-1)


def e4m3fn_bytes(y):
    return np.clip(np.asarray(y, np.float64), -448.0, 448.0).astype(np.float32).astype(ml_dtypes.float8_e4m3fn).view(np.uint8)


Y_SCALE = 160.0


def reference(x, e_enc, W_pre, b_pre):
    out = core(x, e_enc, W_pre, b_pre)
    return out, e4m3fn_bytes(out * Y_SCALE)

@@ -1,0 +1,344 @@
+from contextlib import ExitStack
+
+import concourse.mybir as mybir
+from concourse.masks import make_block_diagonal, make_identity
+
+F32 = mybir.dt.float32
+BF16 = mybir.dt.bfloat16
+I32 = mybir.dt.int32
+U8 = mybir.dt.uint8
+FP8X4 = mybir.dt.float8_e4m3fn_x4
+FP8 = mybir.dt.float8_e4m3fn
+ALU = mybir.AluOpType
+ACT = mybir.ActivationFunctionType
+
+FLOPS = 2 * (4096 + 256) * 1024 * 1024
+
+P = 128
+NJ = 32
+NPR = 16
+F = 1024
+H = 512
+CG = 256
+CV = H - CG
+LEAD = 3
+Y_SCALE = 160.0
+EPS_STD = 1e-5
+INV = 1.0 / 32.0
+
+
+def tile_gnnlayer_pa_kernel(tc, x, e_enc, W_pre, b_pre, out_0, out_1):
+    nc = tc.nc
+    x_rows = x.flatten_outer_dims()
+    e_rows = e_enc.rearrange("b i j k -> (b i) j k")
+    o0 = out_0.flatten_outer_dims().rearrange("p (s f) -> p s f", s=4)
+    o1 = out_1.flatten_outer_dims().rearrange("p (s f) -> p s f", s=4)
+
+    with ExitStack() as ctx:
+        const = ctx.enter_context(tc.tile_pool(name="const", bufs=1))
+        wraw_pool = ctx.enter_context(tc.tile_pool(name="wraw", bufs=4))
+        wgrp_pool = ctx.enter_context(tc.tile_pool(name="wgrp", bufs=2))
+        eraw_pool = ctx.enter_context(tc.tile_pool(name="eraw", bufs=4))
+        egrp_pool = ctx.enter_context(tc.tile_pool(name="egrp", bufs=2))
+        ecod_pool = ctx.enter_context(tc.tile_pool(name="ecod", bufs=3))
+        st_pool = ctx.enter_context(tc.tile_pool(name="st", bufs=5))
+        shr = ctx.enter_context(tc.tile_pool(name="shr", bufs=1))
+        ptp = ctx.enter_context(tc.psum_pool(name="ptp", bufs=2))
+        pz = ctx.enter_context(tc.psum_pool(name="pz", bufs=5))
+        psig = ctx.enter_context(tc.psum_pool(name="psig", bufs=1))
+
+        warm = const.tile([P, 2], F32, name="warm")
+        nc.vector.memset(warm[:, 0:1], 1.0)
+        nc.scalar.activation(out=warm[:, 1:2], in_=warm[:, 0:1], func=ACT.Sqrt)
+        ident = const.tile([P, P], F32, name="ident")
+        make_identity(nc, ident[:])
+        bd = const.tile([P, P], F32, name="bd")
+        make_block_diagonal(nc, bd[:], 32)
+
+        x_sb = const.tile([P, 1024], BF16, name="x_sb")
+        xg = const.tile([P, 1024], BF16, name="xg", align_bytes=64)
+        xg4 = shr.tile([P, 4096], BF16, name="xg4", tag="sha", align_bytes=64)
+        xc = const.tile([P, 256], I32, name="xc", align_bytes=64)
+        xs = const.tile([P, 256], U8, name="xs", align_bytes=64)
+        xc4 = shr.tile([P, 1024], I32, name="xc4", tag="shb", align_bytes=64)
+        xs4 = const.tile([P, 1024], U8, name="xs4", align_bytes=64)
+        xrep_c = const.tile([P, 2, NJ, P], I32, name="xrep_c", align_bytes=64)
+        xrep_s = const.tile([P, 2, NJ, P], U8, name="xrep_s", align_bytes=64)
+        wc = const.tile([P, 3, 2, 2, H], I32, name="wc", align_bytes=64)
+        ws = const.tile([P, 3, 2, 2, H], U8, name="ws", align_bytes=64)
+        b_bc = const.tile([P, F], BF16, name="b_bc")
+        late = {}
+        s_sb = const.tile([P, H], F32, name="s_sb")
+        srep32 = const.tile([P, H], F32, name="srep32")
+        res = const.tile([P, 4, F], F32, name="res")
+        acc_g0 = const.tile([P, CG + H], F32, name="acc_g0")
+        acc_g1 = const.tile([P, H], F32, name="acc_g1")
+        acc_v = const.tile([P, CV], F32, name="acc_v")
+        o8 = const.tile([P, 4, F], FP8, name="o8")
+        sig = psig.tile([P, H], F32, name="sig")
+
+        wraw = {}
+        eraw = {}
+
+        def load_w(w, g, h):
+            t = wraw_pool.tile([P, 4, H], BF16, name="wraw", tag="wraw")
+            r0 = w * 1024 + g * 512
+            nc.sync.dma_start(out=t[:], in_=W_pre[r0 : r0 + 512, H * h : H * (h + 1)].rearrange("(p t) f -> p t f", t=4))
+            wraw[(w, g, h)] = t
+
+        def load_e(pr):
+            t = eraw_pool.tile([P, 2, 1024], BF16, name="eraw", tag="eraw")
+            nc.sync.dma_start(out=t[:], in_=e_rows[:, 2 * pr : 2 * pr + 2, :])
+            eraw[pr] = t
+
+        nc.sync.dma_start(out=x_sb[:], in_=x_rows)
+        for w in (2, 1):
+            for g in range(2):
+                load_w(w, g, 0)
+        for pr in range(4):
+            load_e(pr)
+
+        xt = ptp.tile([P, 4, P], F32, name="tp", tag="tp")
+        xwords = x_sb[:].bitcast(F32)
+        for g in range(2):
+            for u in range(2):
+                nc.tensor.transpose(xt[:, 2 * g + u, :], xwords[:, 256 * g + u : 256 * (g + 1) : 2], ident[:])
+        nc.vector.tensor_copy(
+            out=xg[:].bitcast(F32).rearrange("p (g r u) -> p g r u", g=2, u=2),
+            in_=xt[:].rearrange("p (g u) r -> p g r u", u=2),
+        )
+        nc.vector.memset(xs4[:].bitcast(I32), 0)
+        nc.vector.tensor_copy(
+            out=xg4[:].bitcast(F32).rearrange("p (c i u) -> p c i u", i=4, u=2),
+            in_=xg[:].bitcast(F32).rearrange("p (c u) -> p c u", u=2).unsqueeze(2).to_broadcast([P, 256, 4, 2]),
+        )
+        nc.vector.quantize_mx(out=xc[:].bitcast(FP8X4), scales=xs[:], in_=xg[:])
+        nc.vector.quantize_mx(out=xc4[:].bitcast(FP8X4), scales=xs4[:], in_=xg4[:])
+
+        def replicate_x(j0, j1):
+            for g in range(2):
+                nc.vector.tensor_copy(
+                    out=xrep_c[:, g, j0:j1, :].rearrange("p j (b i) -> p j b i", b=4),
+                    in_=xc[:, 128 * g : 128 * (g + 1)].rearrange("p (b j) -> p j b", b=4)[:, j0:j1, :].unsqueeze(3).to_broadcast([P, j1 - j0, 4, 32]),
+                )
+                nc.vector.tensor_copy(
+                    out=xrep_s[:, g, j0:j1, :].bitcast(I32).rearrange("p j (b r) -> p j b r", b=4),
+                    in_=xs4[:].bitcast(I32)[:, 128 * g : 128 * (g + 1)].rearrange("p (b j) -> p j b", b=4)[:, j0:j1, :].unsqueeze(3).to_broadcast([P, j1 - j0, 4, 8]),
+                )
+
+        replicate_x(0, 8)
+
+        wgrp = {}
+
+        def interleave_w(w, g, h, eng):
+            if (w, h) not in wgrp:
+                wgrp[(w, h)] = wgrp_pool.tile([P, 2, 2048], BF16, name="wgrp", tag="wgrp", align_bytes=64)
+            dst = wgrp[(w, h)][:, g, :].rearrange("p (f t) -> p f t", t=4)
+            src = wraw[(w, g, h)][:].rearrange("p t f -> p f t")
+            if eng == "v":
+                nc.vector.tensor_copy(out=dst, in_=src)
+            elif eng == "s":
+                nc.scalar.copy(out=dst, in_=src)
+            else:
+                nc.gpsimd.tensor_scalar(out=dst, in0=src, scalar1=1.0, scalar2=0.0, op0=ALU.mult, op1=ALU.add)
+
+        def quant_w(w, h, g0, g1):
+            nc.vector.quantize_mx(
+                out=wc[:, w, h, g0:g1, :].rearrange("p g f -> p (g f)").bitcast(FP8X4),
+                scales=ws[:, w, h, g0:g1, :].rearrange("p g f -> p (g f)"),
+                in_=wgrp[(w, h)][:, g0:g1, :].rearrange("p g c -> p (g c)"),
+            )
+
+        tps = {}
+        egrp = {}
+        ecod = {}
+
+        def transposes(pr):
+            raw = eraw[pr]
+            for jj in range(2):
+                tp = ptp.tile([P, 4, P], F32, name="tp", tag="tp")
+                words = raw[:, jj, :].bitcast(F32)
+                for g in range(2):
+                    for u in range(2):
+                        nc.tensor.transpose(tp[:, 2 * g + u, :], words[:, 256 * g + u : 256 * (g + 1) : 2], ident[:])
+                tps[(pr, jj)] = tp
+
+        def copy_out(pr):
+            q = pr // 2
+            if q not in egrp:
+                egrp[q] = egrp_pool.tile([P, 4096], BF16, name="egrp", tag="egrp", align_bytes=64)
+            gw = egrp[q][:].bitcast(F32).rearrange("p (n g r u) -> p n g r u", n=4, g=2, u=2)
+            for jj in range(2):
+                nc.scalar.copy(out=gw[:, 2 * (pr % 2) + jj], in_=tps[(pr, jj)][:].rearrange("p (g u) r -> p g r u", u=2))
+
+        def quant(q, n0, n1):
+            if q not in ecod:
+                ec = ecod_pool.tile([P, 1024], I32, name="ec", tag="ec", align_bytes=64)
+                es = ecod_pool.tile([P, 1024], U8, name="es", tag="es", align_bytes=64)
+                ecod[q] = (ec, es)
+            ec, es = ecod[q]
+            nc.vector.quantize_mx(
+                out=ec[:, 256 * n0 : 256 * n1].bitcast(FP8X4),
+                scales=es[:, 256 * n0 : 256 * n1],
+                in_=egrp[q][:, 1024 * n0 : 1024 * n1],
+            )
+
+        def mx(out, lc, ls, w, h, g, start, stop):
+            nc.tensor.matmul_mx(
+                out=out,
+                lhsT=lc.bitcast(FP8X4),
+                lhsT_scale=ls,
+                rhs=wc[:, w, h, g, :].bitcast(FP8X4),
+                rhs_scale=ws[:, w, h, g, :],
+                start=start,
+                stop=stop,
+            )
+
+        def bank(j, h):
+            ec, es = ecod[j // 4]
+            hs = slice(H * h, H * (h + 1))
+            z = pz.tile([P, H], F32, name="z", tag="z")
+            for g in range(2):
+                a = ((j % 4) * 2 + g) * 128
+                mx(z[:], ec[:, a : a + 128], es[:, a : a + 128], 2, h, g, g == 0, False)
+            for g in range(2):
+                mx(z[:], xrep_c[:, g, j, :], xrep_s[:, g, j, :], 1, h, g, False, g == 1)
+            if h == 1:
+                for g in range(2):
+                    a = ((j % 4) * 2 + g) * 128
+                    mx(sig[:], ec[:, a : a + 128], es[:, a : a + 128], 2, 1, g, j == 0 and g == 0, j == NJ - 1 and g == 1)
+            acc = acc_g0 if h == 0 else acc_g1
+            if j == 0:
+                nc.scalar.copy(out=res[:, 2, hs], in_=z[:])
+                nc.scalar.copy(out=res[:, 1, hs], in_=z[:])
+                dst = acc
+            else:
+                nc.vector.tensor_tensor(out=res[:, 2, hs], in0=z[:], in1=res[:, 2, hs], op=ALU.max)
+                nc.vector.tensor_tensor(out=res[:, 1, hs], in0=z[:], in1=res[:, 1, hs], op=ALU.min)
+                if h == 0:
+                    dst = st_pool.tile([P, CG + H], F32, name="st0", tag="st0")
+                else:
+                    dst = st_pool.tile([P, H], F32, name="st1", tag="st1")
+            if h == 0:
+                nc.scalar.activation(out=dst[:, CG : CG + H], in_=z[:], func=ACT.Square)
+                nc.scalar.copy(out=dst[:, 0:CG], in_=z[:, 0:CG])
+                if j == 0:
+                    nc.vector.tensor_copy(out=acc_v[:], in_=z[:, CG:H])
+                else:
+                    nc.vector.tensor_tensor(out=acc_v[:], in0=z[:, CG:H], in1=acc_v[:], op=ALU.add)
+            else:
+                nc.scalar.activation(out=dst[:], in_=z[:], func=ACT.Square)
+            if j > 0:
+                add = nc.vector.tensor_tensor if (h == 1 and j == NJ - 1) else nc.gpsimd.tensor_tensor
+                add(out=acc[:], in0=acc[:], in1=dst[:], op=ALU.add)
+
+        def small_products():
+            s_ps = pz.tile([P, H], F32, name="z", tag="z")
+            for g in range(2):
+                mx(s_ps[:], xc[:, 128 * g : 128 * (g + 1)], xs[:, 128 * g : 128 * (g + 1)], 1, 1, g, g == 0, g == 1)
+            nc.scalar.copy(out=s_sb[:], in_=s_ps[:])
+            srep_ps = pz.tile([P, H], F32, name="z", tag="z")
+            nc.tensor.matmul(out=srep_ps[:], lhsT=bd[:], rhs=s_sb[:], start=True, stop=True)
+            nc.scalar.activation(out=srep32[:], in_=srep_ps[:], func=ACT.Copy, scale=INV)
+
+        def target_term():
+            base = shr.tile([P, F], F32, name="base", tag="shb", align_bytes=64)
+            late["base"] = base
+            for h in range(2):
+                tg = pz.tile([P, H], F32, name="z", tag="z")
+                for g in range(2):
+                    mx(tg[:], xc[:, 128 * g : 128 * (g + 1)], xs[:, 128 * g : 128 * (g + 1)], 0, h, g, g == 0, g == 1)
+                nc.vector.tensor_tensor(out=base[:, H * h : H * (h + 1)], in0=tg[:], in1=b_bc[:, H * h : H * (h + 1)], op=ALU.add)
+
+        def cast(eng, s, hs):
+            if eng == "s":
+                nc.scalar.activation(out=o8[:, s, hs], in_=res[:, s, hs], func=ACT.Copy, scale=Y_SCALE, saturate=False)
+            else:
+                nc.vector.tensor_scalar(out=o8[:, s, hs], in0=res[:, s, hs], scalar1=Y_SCALE, scalar2=None, op0=ALU.mult, saturate=False)
+
+        def finish(h):
+            base = late["base"]
+            mz = late["mm"][:, 0, :]
+            msq = late["mm"][:, 1, :]
+            hs = slice(H * h, H * (h + 1))
+            if h == 1:
+                nc.vector.scalar_tensor_tensor(out=mz[:, hs], in0=sig[:], scalar=INV, in1=srep32[:], op0=ALU.mult, op1=ALU.add)
+                sq = acc_g1[:]
+            else:
+                nc.scalar.activation(out=mz[:, 0:CG], in_=acc_g0[:, 0:CG], func=ACT.Copy, scale=INV)
+                nc.scalar.activation(out=mz[:, CG:H], in_=acc_v[:], func=ACT.Copy, scale=INV)
+                sq = acc_g0[:, CG : CG + H]
+            nc.scalar.activation(out=msq[:, hs], in_=mz[:, hs], func=ACT.Square)
+            nc.vector.scalar_tensor_tensor(out=msq[:, hs], in0=sq, scalar=INV, in1=msq[:, hs], op0=ALU.mult, op1=ALU.subtract)
+            nc.vector.tensor_scalar(out=msq[:, hs], in0=msq[:, hs], scalar1=0.0, scalar2=EPS_STD, op0=ALU.max, op1=ALU.add)
+            nc.scalar.activation(out=res[:, 3, hs], in_=msq[:, hs], func=ACT.Sqrt)
+            nc.vector.tensor_tensor(out=res[:, 2, hs], in0=res[:, 2, hs], in1=base[:, hs], op=ALU.add)
+            nc.vector.tensor_tensor(out=res[:, 1, hs], in0=res[:, 1, hs], in1=base[:, hs], op=ALU.add)
+            nc.vector.tensor_tensor(out=res[:, 0, hs], in0=mz[:, hs], in1=base[:, hs], op=ALU.add)
+            nc.sync.dma_start(out=o0[:, 0:3, hs], in_=res[:, 0:3, hs])
+            nc.sync.dma_start(out=o0[:, 3, hs], in_=res[:, 3, hs])
+            cast("s", 2, hs)
+            cast("s" if h == 0 else "v", 1, hs)
+            cast("s", 0, hs)
+            cast("s" if h == 0 else "v", 3, hs)
+            nc.sync.dma_start(out=o1[:, 0:3, hs], in_=o8[:, 0:3, hs].bitcast(U8))
+            nc.sync.dma_start(out=o1[:, 3, hs], in_=o8[:, 3, hs].bitcast(U8))
+
+        interleave_w(2, 0, 0, "s")
+        interleave_w(2, 1, 0, "s")
+        interleave_w(1, 0, 0, "s")
+        interleave_w(1, 1, 0, "v")
+        for w in (2, 1):
+            for g in range(2):
+                load_w(w, g, 1)
+        transposes(0)
+        copy_out(0)
+        for w in (2, 1):
+            for g in range(2):
+                quant_w(w, 0, g, g + 1)
+        quant(0, 0, 2)
+        replicate_x(8, NJ)
+        transposes(1)
+        copy_out(1)
+        quant(0, 2, 4)
+
+        for it in range(NPR + LEAD):
+            if it + 2 < NPR:
+                transposes(it + 2)
+                copy_out(it + 2)
+                if it % 2 == 1:
+                    quant((it + 2) // 2, 0, 4)
+            if it + 4 < NPR:
+                load_e(it + 4)
+            for jj in range(2):
+                if it < NPR:
+                    bank(2 * it + jj, 0)
+                if it >= LEAD:
+                    bank(2 * (it - LEAD) + jj, 1)
+            if it == 0:
+                interleave_w(2, 0, 1, "s")
+                interleave_w(2, 1, 1, "s")
+            if it == 1:
+                quant_w(2, 1, 0, 2)
+                interleave_w(1, 0, 1, "s")
+            if it == 2:
+                interleave_w(1, 1, 1, "s")
+                quant_w(1, 1, 0, 2)
+            if it == 1:
+                nc.sync.dma_start(out=b_bc[:], in_=b_pre.partition_broadcast(P))
+            if it == 2:
+                for h in range(2):
+                    for g in range(2):
+                        load_w(0, g, h)
+            if it == 3:
+                small_products()
+            if it in (5, 6, 7, 8):
+                h, g = divmod(it - 5, 2)
+                interleave_w(0, g, h, "s")
+                if g == 1:
+                    quant_w(0, h, 0, 2)
+            if it == 10:
+                target_term()
+        late["mm"] = shr.tile([P, 2, F], F32, name="mm", tag="sha", align_bytes=64)
+        finish(0)
+        finish(1)

@@ -19,9 +19,11 @@ NJ = 32
 NPR = 16
 F = 1024
 H = 512
-CG = 256
-CV = H - CG
-LEAD = 3
+SPLIT = ((256, 192, 64), (256, 192, 64))
+FS = 256
+XR0 = 4
+XR1 = 12
+MANUAL = False
 Y_SCALE = 160.0
 EPS_STD = 1e-5
 INV = 1.0 / 32.0
@@ -33,15 +35,18 @@ def tile_gnnlayer_pa_kernel(tc, x, e_enc, W_pre, b_pre, out_0, out_1):
     e_rows = e_enc.rearrange("b i j k -> (b i) j k")
     o0 = out_0.flatten_outer_dims().rearrange("p (s f) -> p s f", s=4)
     o1 = out_1.flatten_outer_dims().rearrange("p (s f) -> p s f", s=4)
+    sig_off = (0, SPLIT[0][0])
+    sig_w = SPLIT[0][0] + SPLIT[1][0]
 
     with ExitStack() as ctx:
+        if MANUAL:
+            ctx.enter_context(tc.manual_schedule())
         const = ctx.enter_context(tc.tile_pool(name="const", bufs=1))
         wraw_pool = ctx.enter_context(tc.tile_pool(name="wraw", bufs=4))
         wgrp_pool = ctx.enter_context(tc.tile_pool(name="wgrp", bufs=2))
-        eraw_pool = ctx.enter_context(tc.tile_pool(name="eraw", bufs=4))
+        eraw_pool = ctx.enter_context(tc.tile_pool(name="eraw", bufs=3))
         egrp_pool = ctx.enter_context(tc.tile_pool(name="egrp", bufs=2))
-        ecod_pool = ctx.enter_context(tc.tile_pool(name="ecod", bufs=3))
-        st_pool = ctx.enter_context(tc.tile_pool(name="st", bufs=5))
+        st_pool = ctx.enter_context(tc.tile_pool(name="st", bufs=4))
         shr = ctx.enter_context(tc.tile_pool(name="shr", bufs=1))
         ptp = ctx.enter_context(tc.psum_pool(name="ptp", bufs=2))
         pz = ctx.enter_context(tc.psum_pool(name="pz", bufs=5))
@@ -62,20 +67,21 @@ def tile_gnnlayer_pa_kernel(tc, x, e_enc, W_pre, b_pre, out_0, out_1):
         xs = const.tile([P, 256], U8, name="xs", align_bytes=64)
         xc4 = shr.tile([P, 1024], I32, name="xc4", tag="shb", align_bytes=64)
         xs4 = const.tile([P, 1024], U8, name="xs4", align_bytes=64)
-        xrep_c = const.tile([P, 2, NJ, P], I32, name="xrep_c", align_bytes=64)
-        xrep_s = const.tile([P, 2, NJ, P], U8, name="xrep_s", align_bytes=64)
+        xrep_c = const.tile([P, NJ, 2, P], I32, name="xrep_c", align_bytes=64)
+        xrep_s = const.tile([P, NJ, 2, P], U8, name="xrep_s", align_bytes=64)
         wc = const.tile([P, 3, 2, 2, H], I32, name="wc", align_bytes=64)
         ws = const.tile([P, 3, 2, 2, H], U8, name="ws", align_bytes=64)
+        ec = const.tile([P, NJ, 256], I32, name="ec", align_bytes=64)
+        es = const.tile([P, NJ, 256], U8, name="es", align_bytes=64)
         b_bc = const.tile([P, F], BF16, name="b_bc")
         late = {}
-        s_sb = const.tile([P, H], F32, name="s_sb")
-        srep32 = const.tile([P, H], F32, name="srep32")
+        s_sb = const.tile([P, sig_w], F32, name="s_sb")
+        srep32 = const.tile([P, sig_w], F32, name="srep32")
         res = const.tile([P, 4, F], F32, name="res")
-        acc_g0 = const.tile([P, CG + H], F32, name="acc_g0")
-        acc_g1 = const.tile([P, H], F32, name="acc_g1")
-        acc_v = const.tile([P, CV], F32, name="acc_v")
+        acc_g = [const.tile([P, H + SPLIT[h][2]], F32, name="acc_g%d" % h) for h in range(2)]
+        acc_v = [const.tile([P, SPLIT[h][1]], F32, name="acc_v%d" % h) for h in range(2)]
         o8 = const.tile([P, 4, F], FP8, name="o8")
-        sig = psig.tile([P, H], F32, name="sig")
+        sig = {0: psig.tile([P, H], F32, name="sig")}
 
         wraw = {}
         eraw = {}
@@ -91,56 +97,27 @@ def tile_gnnlayer_pa_kernel(tc, x, e_enc, W_pre, b_pre, out_0, out_1):
             nc.sync.dma_start(out=t[:], in_=e_rows[:, 2 * pr : 2 * pr + 2, :])
             eraw[pr] = t
 
-        nc.sync.dma_start(out=x_sb[:], in_=x_rows)
-        for w in (2, 1):
-            for g in range(2):
-                load_w(w, g, 0)
-        for pr in range(4):
-            load_e(pr)
-
-        xt = ptp.tile([P, 4, P], F32, name="tp", tag="tp")
-        xwords = x_sb[:].bitcast(F32)
-        for g in range(2):
-            for u in range(2):
-                nc.tensor.transpose(xt[:, 2 * g + u, :], xwords[:, 256 * g + u : 256 * (g + 1) : 2], ident[:])
-        nc.vector.tensor_copy(
-            out=xg[:].bitcast(F32).rearrange("p (g r u) -> p g r u", g=2, u=2),
-            in_=xt[:].rearrange("p (g u) r -> p g r u", u=2),
-        )
-        nc.vector.memset(xs4[:].bitcast(I32), 0)
-        nc.vector.tensor_copy(
-            out=xg4[:].bitcast(F32).rearrange("p (c i u) -> p c i u", i=4, u=2),
-            in_=xg[:].bitcast(F32).rearrange("p (c u) -> p c u", u=2).unsqueeze(2).to_broadcast([P, 256, 4, 2]),
-        )
-        nc.vector.quantize_mx(out=xc[:].bitcast(FP8X4), scales=xs[:], in_=xg[:])
-        nc.vector.quantize_mx(out=xc4[:].bitcast(FP8X4), scales=xs4[:], in_=xg4[:])
-
         def replicate_x(j0, j1):
-            for g in range(2):
-                nc.vector.tensor_copy(
-                    out=xrep_c[:, g, j0:j1, :].rearrange("p j (b i) -> p j b i", b=4),
-                    in_=xc[:, 128 * g : 128 * (g + 1)].rearrange("p (b j) -> p j b", b=4)[:, j0:j1, :].unsqueeze(3).to_broadcast([P, j1 - j0, 4, 32]),
-                )
-                nc.vector.tensor_copy(
-                    out=xrep_s[:, g, j0:j1, :].bitcast(I32).rearrange("p j (b r) -> p j b r", b=4),
-                    in_=xs4[:].bitcast(I32)[:, 128 * g : 128 * (g + 1)].rearrange("p (b j) -> p j b", b=4)[:, j0:j1, :].unsqueeze(3).to_broadcast([P, j1 - j0, 4, 8]),
-                )
-
-        replicate_x(0, 8)
+            nc.vector.tensor_copy(
+                out=xrep_c[:, j0:j1, :, :].rearrange("p j g (b i) -> p j (g b) i", b=4),
+                in_=xc[:].rearrange("p (c j) -> p j c", c=8)[:, j0:j1, :].unsqueeze(3).to_broadcast([P, j1 - j0, 8, 32]),
+            )
+            nc.vector.tensor_copy(
+                out=xrep_s[:, j0:j1, :, :].rearrange("p j g r -> p j (g r)").bitcast(I32).rearrange("p j (c r) -> p j c r", c=8),
+                in_=xs4[:].bitcast(I32).rearrange("p (c j) -> p j c", c=8)[:, j0:j1, :].unsqueeze(3).to_broadcast([P, j1 - j0, 8, 8]),
+            )
 
         wgrp = {}
 
-        def interleave_w(w, g, h, eng):
+        def interleave_w(w, g, h, eng, f0=0, f1=H):
             if (w, h) not in wgrp:
                 wgrp[(w, h)] = wgrp_pool.tile([P, 2, 2048], BF16, name="wgrp", tag="wgrp", align_bytes=64)
-            dst = wgrp[(w, h)][:, g, :].rearrange("p (f t) -> p f t", t=4)
-            src = wraw[(w, g, h)][:].rearrange("p t f -> p f t")
+            dst = wgrp[(w, h)][:, g, 4 * f0 : 4 * f1].rearrange("p (f t) -> p f t", t=4)
+            src = wraw[(w, g, h)][:, :, f0:f1].rearrange("p t f -> p f t")
             if eng == "v":
                 nc.vector.tensor_copy(out=dst, in_=src)
-            elif eng == "s":
-                nc.scalar.copy(out=dst, in_=src)
             else:
-                nc.gpsimd.tensor_scalar(out=dst, in0=src, scalar1=1.0, scalar2=0.0, op0=ALU.mult, op1=ALU.add)
+                nc.scalar.copy(out=dst, in_=src)
 
         def quant_w(w, h, g0, g1):
             nc.vector.quantize_mx(
@@ -151,12 +128,14 @@ def tile_gnnlayer_pa_kernel(tc, x, e_enc, W_pre, b_pre, out_0, out_1):
 
         tps = {}
         egrp = {}
-        ecod = {}
 
-        def transposes(pr):
+        def transposes(pr, head=False):
             raw = eraw[pr]
             for jj in range(2):
-                tp = ptp.tile([P, 4, P], F32, name="tp", tag="tp")
+                if head:
+                    tp = pz.tile([P, 4, P], F32, name="z", tag="z")
+                else:
+                    tp = ptp.tile([P, 4, P], F32, name="tp", tag="tp")
                 words = raw[:, jj, :].bitcast(F32)
                 for g in range(2):
                     for u in range(2):
@@ -172,74 +151,60 @@ def tile_gnnlayer_pa_kernel(tc, x, e_enc, W_pre, b_pre, out_0, out_1):
                 nc.scalar.copy(out=gw[:, 2 * (pr % 2) + jj], in_=tps[(pr, jj)][:].rearrange("p (g u) r -> p g r u", u=2))
 
         def quant(q, n0, n1):
-            if q not in ecod:
-                ec = ecod_pool.tile([P, 1024], I32, name="ec", tag="ec", align_bytes=64)
-                es = ecod_pool.tile([P, 1024], U8, name="es", tag="es", align_bytes=64)
-                ecod[q] = (ec, es)
-            ec, es = ecod[q]
             nc.vector.quantize_mx(
-                out=ec[:, 256 * n0 : 256 * n1].bitcast(FP8X4),
-                scales=es[:, 256 * n0 : 256 * n1],
+                out=ec[:, 4 * q + n0 : 4 * q + n1, :].rearrange("p j c -> p (j c)").bitcast(FP8X4),
+                scales=es[:, 4 * q + n0 : 4 * q + n1, :].rearrange("p j c -> p (j c)"),
                 in_=egrp[q][:, 1024 * n0 : 1024 * n1],
             )
 
-        def mx(out, lc, ls, w, h, g, start, stop):
+        def mx(out, lc, ls, w, h, g, n, start, stop):
             nc.tensor.matmul_mx(
                 out=out,
                 lhsT=lc.bitcast(FP8X4),
                 lhsT_scale=ls,
-                rhs=wc[:, w, h, g, :].bitcast(FP8X4),
-                rhs_scale=ws[:, w, h, g, :],
+                rhs=wc[:, w, h, g, 0:n].bitcast(FP8X4),
+                rhs_scale=ws[:, w, h, g, 0:n],
                 start=start,
                 stop=stop,
             )
 
         def bank(j, h):
-            ec, es = ecod[j // 4]
+            a_t, b_v, c_g = SPLIT[h]
             hs = slice(H * h, H * (h + 1))
             z = pz.tile([P, H], F32, name="z", tag="z")
             for g in range(2):
-                a = ((j % 4) * 2 + g) * 128
-                mx(z[:], ec[:, a : a + 128], es[:, a : a + 128], 2, h, g, g == 0, False)
+                mx(z[:], ec[:, j, 128 * g : 128 * (g + 1)], es[:, j, 128 * g : 128 * (g + 1)], 2, h, g, H, g == 0, False)
             for g in range(2):
-                mx(z[:], xrep_c[:, g, j, :], xrep_s[:, g, j, :], 1, h, g, False, g == 1)
-            if h == 1:
-                for g in range(2):
-                    a = ((j % 4) * 2 + g) * 128
-                    mx(sig[:], ec[:, a : a + 128], es[:, a : a + 128], 2, 1, g, j == 0 and g == 0, j == NJ - 1 and g == 1)
-            acc = acc_g0 if h == 0 else acc_g1
+                mx(z[:], xrep_c[:, j, g, :], xrep_s[:, j, g, :], 1, h, g, H, False, g == 1)
+            for g in range(2):
+                mx(sig[h][:, 0:a_t], ec[:, j, 128 * g : 128 * (g + 1)], es[:, j, 128 * g : 128 * (g + 1)], 2, h, g, a_t, j == 0 and g == 0, j == NJ - 1 and g == 1)
+            if j == 0:
+                dst = acc_g[h]
+            else:
+                dst = st_pool.tile([P, H + c_g], F32, name="st", tag="st")
+            nc.scalar.activation(out=dst[:, 0:H], in_=z[:], func=ACT.Square)
+            if c_g:
+                nc.scalar.copy(out=dst[:, H : H + c_g], in_=z[:, H - c_g : H])
             if j == 0:
                 nc.scalar.copy(out=res[:, 2, hs], in_=z[:])
                 nc.scalar.copy(out=res[:, 1, hs], in_=z[:])
-                dst = acc
+                nc.vector.tensor_copy(out=acc_v[h][:], in_=z[:, a_t : a_t + b_v])
             else:
                 nc.vector.tensor_tensor(out=res[:, 2, hs], in0=z[:], in1=res[:, 2, hs], op=ALU.max)
                 nc.vector.tensor_tensor(out=res[:, 1, hs], in0=z[:], in1=res[:, 1, hs], op=ALU.min)
-                if h == 0:
-                    dst = st_pool.tile([P, CG + H], F32, name="st0", tag="st0")
-                else:
-                    dst = st_pool.tile([P, H], F32, name="st1", tag="st1")
-            if h == 0:
-                nc.scalar.activation(out=dst[:, CG : CG + H], in_=z[:], func=ACT.Square)
-                nc.scalar.copy(out=dst[:, 0:CG], in_=z[:, 0:CG])
-                if j == 0:
-                    nc.vector.tensor_copy(out=acc_v[:], in_=z[:, CG:H])
-                else:
-                    nc.vector.tensor_tensor(out=acc_v[:], in0=z[:, CG:H], in1=acc_v[:], op=ALU.add)
-            else:
-                nc.scalar.activation(out=dst[:], in_=z[:], func=ACT.Square)
-            if j > 0:
+                nc.vector.tensor_tensor(out=acc_v[h][:], in0=z[:, a_t : a_t + b_v], in1=acc_v[h][:], op=ALU.add)
                 add = nc.vector.tensor_tensor if (h == 1 and j == NJ - 1) else nc.gpsimd.tensor_tensor
-                add(out=acc[:], in0=acc[:], in1=dst[:], op=ALU.add)
+                add(out=acc_g[h][:], in0=acc_g[h][:], in1=dst[:], op=ALU.add)
 
         def small_products():
             s_ps = pz.tile([P, H], F32, name="z", tag="z")
-            for g in range(2):
-                mx(s_ps[:], xc[:, 128 * g : 128 * (g + 1)], xs[:, 128 * g : 128 * (g + 1)], 1, 1, g, g == 0, g == 1)
-            nc.scalar.copy(out=s_sb[:], in_=s_ps[:])
+            for h in range(2):
+                for g in range(2):
+                    mx(s_ps[:, sig_off[h] : sig_off[h] + SPLIT[h][0]], xc[:, 128 * g : 128 * (g + 1)], xs[:, 128 * g : 128 * (g + 1)], 1, h, g, SPLIT[h][0], g == 0, g == 1)
+            nc.scalar.copy(out=s_sb[:], in_=s_ps[:, 0:sig_w])
             srep_ps = pz.tile([P, H], F32, name="z", tag="z")
-            nc.tensor.matmul(out=srep_ps[:], lhsT=bd[:], rhs=s_sb[:], start=True, stop=True)
-            nc.scalar.activation(out=srep32[:], in_=srep_ps[:], func=ACT.Copy, scale=INV)
+            nc.tensor.matmul(out=srep_ps[:, 0:sig_w], lhsT=bd[:], rhs=s_sb[:], start=True, stop=True)
+            nc.scalar.activation(out=srep32[:], in_=srep_ps[:, 0:sig_w], func=ACT.Copy, scale=INV)
 
         def target_term():
             base = shr.tile([P, F], F32, name="base", tag="shb", align_bytes=64)
@@ -247,7 +212,7 @@ def tile_gnnlayer_pa_kernel(tc, x, e_enc, W_pre, b_pre, out_0, out_1):
             for h in range(2):
                 tg = pz.tile([P, H], F32, name="z", tag="z")
                 for g in range(2):
-                    mx(tg[:], xc[:, 128 * g : 128 * (g + 1)], xs[:, 128 * g : 128 * (g + 1)], 0, h, g, g == 0, g == 1)
+                    mx(tg[:], xc[:, 128 * g : 128 * (g + 1)], xs[:, 128 * g : 128 * (g + 1)], 0, h, g, H, g == 0, g == 1)
                 nc.vector.tensor_tensor(out=base[:, H * h : H * (h + 1)], in0=tg[:], in1=b_bc[:, H * h : H * (h + 1)], op=ALU.add)
 
         def cast(eng, s, hs):
@@ -256,89 +221,156 @@ def tile_gnnlayer_pa_kernel(tc, x, e_enc, W_pre, b_pre, out_0, out_1):
             else:
                 nc.vector.tensor_scalar(out=o8[:, s, hs], in0=res[:, s, hs], scalar1=Y_SCALE, scalar2=None, op0=ALU.mult, saturate=False)
 
-        def finish(h):
+        def finish_steps(h):
+            a_t, b_v, c_g = SPLIT[h]
             base = late["base"]
             mz = late["mm"][:, 0, :]
             msq = late["mm"][:, 1, :]
-            hs = slice(H * h, H * (h + 1))
-            if h == 1:
-                nc.vector.scalar_tensor_tensor(out=mz[:, hs], in0=sig[:], scalar=INV, in1=srep32[:], op0=ALU.mult, op1=ALU.add)
-                sq = acc_g1[:]
-            else:
-                nc.scalar.activation(out=mz[:, 0:CG], in_=acc_g0[:, 0:CG], func=ACT.Copy, scale=INV)
-                nc.scalar.activation(out=mz[:, CG:H], in_=acc_v[:], func=ACT.Copy, scale=INV)
-                sq = acc_g0[:, CG : CG + H]
-            nc.scalar.activation(out=msq[:, hs], in_=mz[:, hs], func=ACT.Square)
-            nc.vector.scalar_tensor_tensor(out=msq[:, hs], in0=sq, scalar=INV, in1=msq[:, hs], op0=ALU.mult, op1=ALU.subtract)
-            nc.vector.tensor_scalar(out=msq[:, hs], in0=msq[:, hs], scalar1=0.0, scalar2=EPS_STD, op0=ALU.max, op1=ALU.add)
-            nc.scalar.activation(out=res[:, 3, hs], in_=msq[:, hs], func=ACT.Sqrt)
-            nc.vector.tensor_tensor(out=res[:, 2, hs], in0=res[:, 2, hs], in1=base[:, hs], op=ALU.add)
-            nc.vector.tensor_tensor(out=res[:, 1, hs], in0=res[:, 1, hs], in1=base[:, hs], op=ALU.add)
-            nc.vector.tensor_tensor(out=res[:, 0, hs], in0=mz[:, hs], in1=base[:, hs], op=ALU.add)
-            nc.sync.dma_start(out=o0[:, 0:3, hs], in_=res[:, 0:3, hs])
-            nc.sync.dma_start(out=o0[:, 3, hs], in_=res[:, 3, hs])
-            cast("s", 2, hs)
-            cast("s" if h == 0 else "v", 1, hs)
-            cast("s", 0, hs)
-            cast("s" if h == 0 else "v", 3, hs)
-            nc.sync.dma_start(out=o1[:, 0:3, hs], in_=o8[:, 0:3, hs].bitcast(U8))
-            nc.sync.dma_start(out=o1[:, 3, hs], in_=o8[:, 3, hs].bitcast(U8))
+            c0 = H * h
+            hs = slice(c0, c0 + H)
 
-        interleave_w(2, 0, 0, "s")
-        interleave_w(2, 1, 0, "s")
-        interleave_w(1, 0, 0, "s")
-        interleave_w(1, 1, 0, "v")
+            def s1():
+                nc.vector.scalar_tensor_tensor(
+                    out=mz[:, c0 : c0 + a_t], in0=sig[h][:, 0:a_t], scalar=INV, in1=srep32[:, sig_off[h] : sig_off[h] + a_t], op0=ALU.mult, op1=ALU.add
+                )
+                nc.scalar.activation(out=mz[:, c0 + a_t : c0 + a_t + b_v], in_=acc_v[h][:], func=ACT.Copy, scale=INV)
+                if c_g:
+                    nc.scalar.activation(out=mz[:, c0 + H - c_g : c0 + H], in_=acc_g[h][:, H : H + c_g], func=ACT.Copy, scale=INV)
+
+            def s2():
+                nc.scalar.activation(out=msq[:, hs], in_=mz[:, hs], func=ACT.Square)
+
+            def s3():
+                nc.vector.scalar_tensor_tensor(out=msq[:, hs], in0=acc_g[h][:, 0:H], scalar=INV, in1=msq[:, hs], op0=ALU.mult, op1=ALU.subtract)
+                nc.vector.tensor_scalar(out=msq[:, hs], in0=msq[:, hs], scalar1=0.0, scalar2=EPS_STD, op0=ALU.max, op1=ALU.add)
+
+            def s4():
+                nc.scalar.activation(out=res[:, 3, hs], in_=msq[:, hs], func=ACT.Sqrt)
+                nc.vector.tensor_tensor(out=res[:, 2, hs], in0=res[:, 2, hs], in1=base[:, hs], op=ALU.add)
+
+            def s5():
+                nc.sync.dma_start(out=o0[:, 3, hs], in_=res[:, 3, hs])
+                cast("s", 3, hs)
+                nc.vector.tensor_tensor(out=res[:, 1, hs], in0=res[:, 1, hs], in1=base[:, hs], op=ALU.add)
+
+            def s6():
+                nc.sync.dma_start(out=o1[:, 3, hs], in_=o8[:, 3, hs].bitcast(U8))
+                cast("s", 2, hs)
+                nc.vector.tensor_tensor(out=res[:, 0, hs], in0=mz[:, hs], in1=base[:, hs], op=ALU.add)
+
+            def s7():
+                nc.sync.dma_start(out=o0[:, 0:3, hs], in_=res[:, 0:3, hs])
+                cast("s" if h == 0 else "v", 1, hs)
+                cast("s", 0, hs)
+
+            def s8():
+                nc.sync.dma_start(out=o1[:, 0:3, hs], in_=o8[:, 0:3, hs].bitcast(U8))
+
+            return [s1, s2, s3, s4, s5, s6, s7, s8]
+
+        nc.sync.dma_start(out=x_sb[:], in_=x_rows)
+        load_e(0)
         for w in (2, 1):
             for g in range(2):
-                load_w(w, g, 1)
-        transposes(0)
+                load_w(w, g, 0)
+        load_e(1)
+        load_e(2)
+
+        nc.vector.memset(xs4[:].bitcast(I32), 0)
+        xt = ptp.tile([P, 4, P], F32, name="tp", tag="tp")
+        xwords = x_sb[:].bitcast(F32)
+        for g in range(2):
+            for u in range(2):
+                nc.tensor.transpose(xt[:, 2 * g + u, :], xwords[:, 256 * g + u : 256 * (g + 1) : 2], ident[:])
+        nc.scalar.copy(
+            out=xg[:].bitcast(F32).rearrange("p (g r u) -> p g r u", g=2, u=2),
+            in_=xt[:].rearrange("p (g u) r -> p g r u", u=2),
+        )
+        transposes(0, head=True)
         copy_out(0)
-        for w in (2, 1):
-            for g in range(2):
-                quant_w(w, 0, g, g + 1)
+        nc.vector.quantize_mx(out=xc[:].bitcast(FP8X4), scales=xs[:], in_=xg[:])
+        nc.vector.tensor_copy(
+            out=xg4[:].bitcast(F32).rearrange("p (c i u) -> p c i u", i=4, u=2),
+            in_=xg[:].bitcast(F32).rearrange("p (c u) -> p c u", u=2).unsqueeze(2).to_broadcast([P, 256, 4, 2]),
+        )
+        nc.vector.quantize_mx(out=xc4[:].bitcast(FP8X4), scales=xs4[:], in_=xg4[:])
+        interleave_w(2, 0, 0, "v", 0, FS)
+        interleave_w(2, 0, 0, "s", FS, H)
         quant(0, 0, 2)
-        replicate_x(8, NJ)
-        transposes(1)
+        quant_w(2, 0, 0, 1)
+        interleave_w(2, 1, 0, "v", 0, FS)
+        interleave_w(2, 1, 0, "s", FS, H)
+        quant_w(2, 0, 1, 2)
+        replicate_x(0, XR0)
+        interleave_w(1, 0, 0, "v", 0, FS)
+        interleave_w(1, 0, 0, "s", FS, H)
+        quant_w(1, 0, 0, 1)
+        interleave_w(1, 1, 0, "v", 0, FS)
+        interleave_w(1, 1, 0, "s", FS, H)
+        quant_w(1, 0, 1, 2)
+        transposes(1, head=True)
         copy_out(1)
-        quant(0, 2, 4)
+        load_e(3)
+        load_e(4)
+        load_w(2, 0, 1)
+        load_w(2, 1, 1)
 
-        for it in range(NPR + LEAD):
-            if it + 2 < NPR:
-                transposes(it + 2)
-                copy_out(it + 2)
-                if it % 2 == 1:
-                    quant((it + 2) // 2, 0, 4)
-            if it + 4 < NPR:
-                load_e(it + 4)
-            for jj in range(2):
-                if it < NPR:
-                    bank(2 * it + jj, 0)
-                if it >= LEAD:
-                    bank(2 * (it - LEAD) + jj, 1)
-            if it == 0:
-                interleave_w(2, 0, 1, "s")
-                interleave_w(2, 1, 1, "s")
-            if it == 1:
-                quant_w(2, 1, 0, 2)
-                interleave_w(1, 0, 1, "s")
-            if it == 2:
-                interleave_w(1, 1, 1, "s")
-                quant_w(1, 1, 0, 2)
-            if it == 1:
+        w_later = [(2, 0, 1), (2, 1, 1), (1, 0, 1), (1, 1, 1), (0, 0, 0), (0, 1, 0), (0, 0, 1), (0, 1, 1)]
+        tr_after = {0: 2, 1: 3, 2: 4, 3: 5}
+        for n in range(5, NJ, 2):
+            if (n + 7) // 2 < NPR:
+                tr_after[n] = (n + 7) // 2
+        loads_after = {0: [("e", 5)], 1: [("e", 6), ("w", 1, 0, 1), ("w", 1, 1, 1)], 2: [("e", 7)], 3: [("e", 8)], 9: [("w", 0, 0, 0), ("w", 0, 1, 0)], 17: [("w", 0, 0, 1), ("w", 0, 1, 1)]}
+        for n in range(5, NJ, 2):
+            if (n + 7) // 2 + 3 < NPR:
+                loads_after.setdefault(n, []).append(("e", (n + 7) // 2 + 3))
+        v_after = {0: [("qe", 0, 2, 4)], 1: [("xr", XR0, XR1)], 3: [("qe", 1, 0, 4)], 4: [("qe", 2, 0, 4)], 6: [("xr", XR1, NJ)]}
+        for q in range(3, 8):
+            v_after.setdefault(4 * q - 4, []).append(("qe", q, 0, 4))
+        for i in range(3):
+            v_after.setdefault(8 * i + 11, []).append(("qw",) + (w_later[2 * i][0], w_later[2 * i][2]))
+
+        def il_piece(n):
+            w, g, h = w_later[n // 2]
+            interleave_w(w, g, h, "s", 256 * (n % 2), 256 * (n % 2 + 1))
+
+        for j in range(NJ):
+            bank(j, 0)
+            if j % 2 == 0 and j >= 4:
+                il_piece(j // 2 - 2)
+            for a in v_after.get(j, []):
+                if a[0] == "qe":
+                    quant(a[1], a[2], a[3])
+                elif a[0] == "xr":
+                    replicate_x(a[1], a[2])
+                else:
+                    quant_w(a[1], a[2], 0, 2)
+            if j in tr_after:
+                transposes(tr_after[j])
+                copy_out(tr_after[j])
+            for a in loads_after.get(j, []):
+                if a[0] == "e":
+                    load_e(a[1])
+                else:
+                    load_w(a[1], a[2], a[3])
+            if j == 4:
                 nc.sync.dma_start(out=b_bc[:], in_=b_pre.partition_broadcast(P))
-            if it == 2:
-                for h in range(2):
-                    for g in range(2):
-                        load_w(0, g, h)
-            if it == 3:
+            if j == 21:
                 small_products()
-            if it in (5, 6, 7, 8):
-                h, g = divmod(it - 5, 2)
-                interleave_w(0, g, h, "s")
-                if g == 1:
-                    quant_w(0, h, 0, 2)
-            if it == 10:
-                target_term()
+
+        sig[1] = ptp.tile([P, H], F32, name="tp", tag="tp")
         late["mm"] = shr.tile([P, 2, F], F32, name="mm", tag="sha", align_bytes=64)
-        finish(0)
-        finish(1)
+        steps = []
+        for j in range(NJ):
+            bank(j, 1)
+            if j in (0, 2):
+                il_piece(14 + j // 2)
+            if j == 3:
+                quant_w(0, 1, 0, 2)
+            if j == 4:
+                target_term()
+                steps = finish_steps(0)
+            if j >= 6 and steps:
+                steps.pop(0)()
+        for s in finish_steps(1):
+            s()

@@ -77,10 +77,10 @@ def tile_gnnlayer_pa_kernel(tc, x, e_enc, W_pre, b_pre, out_0, out_1):
         late = {}
         s_sb = const.tile([P, sig_w], F32, name="s_sb")
         srep32 = const.tile([P, sig_w], F32, name="srep32")
-        res = const.tile([P, 4, F], F32, name="res")
+        res = [const.tile([P, 4, H], F32, name="res%d" % h) for h in range(2)]
         acc_g = [const.tile([P, H + SPLIT[h][2]], F32, name="acc_g%d" % h) for h in range(2)]
         acc_v = [const.tile([P, SPLIT[h][1]], F32, name="acc_v%d" % h) for h in range(2)]
-        o8 = const.tile([P, 4, F], FP8, name="o8")
+        o8 = [const.tile([P, 4, H], FP8, name="o8%d" % h) for h in range(2)]
         sig = {0: psig.tile([P, H], F32, name="sig")}
 
         wraw = {}
@@ -186,87 +186,97 @@ def tile_gnnlayer_pa_kernel(tc, x, e_enc, W_pre, b_pre, out_0, out_1):
             if c_g:
                 nc.scalar.copy(out=dst[:, H : H + c_g], in_=z[:, H - c_g : H])
             if j == 0:
-                nc.scalar.copy(out=res[:, 2, hs], in_=z[:])
-                nc.scalar.copy(out=res[:, 1, hs], in_=z[:])
+                nc.scalar.copy(out=res[h][:, 2, :], in_=z[:])
+                nc.scalar.copy(out=res[h][:, 1, :], in_=z[:])
                 nc.vector.tensor_copy(out=acc_v[h][:], in_=z[:, a_t : a_t + b_v])
             else:
-                nc.vector.tensor_tensor(out=res[:, 2, hs], in0=z[:], in1=res[:, 2, hs], op=ALU.max)
-                nc.vector.tensor_tensor(out=res[:, 1, hs], in0=z[:], in1=res[:, 1, hs], op=ALU.min)
+                nc.vector.tensor_tensor(out=res[h][:, 2, :], in0=z[:], in1=res[h][:, 2, :], op=ALU.max)
+                nc.vector.tensor_tensor(out=res[h][:, 1, :], in0=z[:], in1=res[h][:, 1, :], op=ALU.min)
                 nc.vector.tensor_tensor(out=acc_v[h][:], in0=z[:, a_t : a_t + b_v], in1=acc_v[h][:], op=ALU.add)
                 add = nc.vector.tensor_tensor if (h == 1 and j == NJ - 1) else nc.gpsimd.tensor_tensor
                 add(out=acc_g[h][:], in0=acc_g[h][:], in1=dst[:], op=ALU.add)
 
-        def small_products():
+        def source_sum_a():
             s_ps = pz.tile([P, H], F32, name="z", tag="z")
             for h in range(2):
                 for g in range(2):
                     mx(s_ps[:, sig_off[h] : sig_off[h] + SPLIT[h][0]], xc[:, 128 * g : 128 * (g + 1)], xs[:, 128 * g : 128 * (g + 1)], 1, h, g, SPLIT[h][0], g == 0, g == 1)
             nc.scalar.copy(out=s_sb[:], in_=s_ps[:, 0:sig_w])
+
+        def source_sum_b():
             srep_ps = pz.tile([P, H], F32, name="z", tag="z")
             nc.tensor.matmul(out=srep_ps[:, 0:sig_w], lhsT=bd[:], rhs=s_sb[:], start=True, stop=True)
             nc.scalar.activation(out=srep32[:], in_=srep_ps[:, 0:sig_w], func=ACT.Copy, scale=INV)
 
-        def target_term():
-            base = shr.tile([P, F], F32, name="base", tag="shb", align_bytes=64)
-            late["base"] = base
-            for h in range(2):
-                tg = pz.tile([P, H], F32, name="z", tag="z")
-                for g in range(2):
-                    mx(tg[:], xc[:, 128 * g : 128 * (g + 1)], xs[:, 128 * g : 128 * (g + 1)], 0, h, g, H, g == 0, g == 1)
-                nc.vector.tensor_tensor(out=base[:, H * h : H * (h + 1)], in0=tg[:], in1=b_bc[:, H * h : H * (h + 1)], op=ALU.add)
+        def target_term(h):
+            if "base" not in late:
+                late["base"] = shr.tile([P, F], F32, name="base", tag="shb", align_bytes=64)
+            tg = pz.tile([P, H], F32, name="z", tag="z")
+            for g in range(2):
+                mx(tg[:], xc[:, 128 * g : 128 * (g + 1)], xs[:, 128 * g : 128 * (g + 1)], 0, h, g, H, g == 0, g == 1)
+            nc.vector.tensor_tensor(out=late["base"][:, H * h : H * (h + 1)], in0=tg[:], in1=b_bc[:, H * h : H * (h + 1)], op=ALU.add)
 
-        def cast(eng, s, hs):
+        def cast(eng, s, h):
             if eng == "s":
-                nc.scalar.activation(out=o8[:, s, hs], in_=res[:, s, hs], func=ACT.Copy, scale=Y_SCALE, saturate=False)
+                nc.scalar.activation(out=o8[h][:, s, :], in_=res[h][:, s, :], func=ACT.Copy, scale=Y_SCALE, saturate=False)
             else:
-                nc.vector.tensor_scalar(out=o8[:, s, hs], in0=res[:, s, hs], scalar1=Y_SCALE, scalar2=None, op0=ALU.mult, saturate=False)
+                nc.vector.tensor_scalar(out=o8[h][:, s, :], in0=res[h][:, s, :], scalar1=Y_SCALE, scalar2=None, op0=ALU.mult, saturate=False)
 
         def finish_steps(h):
             a_t, b_v, c_g = SPLIT[h]
-            base = late["base"]
-            mz = late["mm"][:, 0, :]
-            msq = late["mm"][:, 1, :]
+            d = late["mm"][:, 0, :]
+            q = late["mm"][:, 1, :]
             c0 = H * h
             hs = slice(c0, c0 + H)
 
-            def s1():
+            def mean_t():
                 nc.vector.scalar_tensor_tensor(
-                    out=mz[:, c0 : c0 + a_t], in0=sig[h][:, 0:a_t], scalar=INV, in1=srep32[:, sig_off[h] : sig_off[h] + a_t], op0=ALU.mult, op1=ALU.add
+                    out=res[h][:, 0, 0:a_t], in0=sig[h][:, 0:a_t], scalar=INV, in1=srep32[:, sig_off[h] : sig_off[h] + a_t], op0=ALU.mult, op1=ALU.add
                 )
-                nc.scalar.activation(out=mz[:, c0 + a_t : c0 + a_t + b_v], in_=acc_v[h][:], func=ACT.Copy, scale=INV)
+
+            def mean_vg():
+                nc.scalar.activation(out=res[h][:, 0, a_t : a_t + b_v], in_=acc_v[h][:], func=ACT.Copy, scale=INV)
                 if c_g:
-                    nc.scalar.activation(out=mz[:, c0 + H - c_g : c0 + H], in_=acc_g[h][:, H : H + c_g], func=ACT.Copy, scale=INV)
+                    nc.scalar.activation(out=res[h][:, 0, H - c_g : H], in_=acc_g[h][:, H : H + c_g], func=ACT.Copy, scale=INV)
 
-            def s2():
-                nc.scalar.activation(out=msq[:, hs], in_=mz[:, hs], func=ACT.Square)
+            def mean_sq():
+                nc.scalar.activation(out=d[:, hs], in_=res[h][:, 0, :], func=ACT.Square)
+                if h == 0:
+                    nc.scalar.activation(out=q[:, hs], in_=acc_g[h][:, 0:H], func=ACT.Copy, scale=INV)
 
-            def s3():
-                nc.vector.scalar_tensor_tensor(out=msq[:, hs], in0=acc_g[h][:, 0:H], scalar=INV, in1=msq[:, hs], op0=ALU.mult, op1=ALU.subtract)
-                nc.vector.tensor_scalar(out=msq[:, hs], in0=msq[:, hs], scalar1=0.0, scalar2=EPS_STD, op0=ALU.max, op1=ALU.add)
+            def var():
+                if h == 0:
+                    nc.gpsimd.tensor_tensor(out=d[:, hs], in0=q[:, hs], in1=d[:, hs], op=ALU.subtract)
+                    nc.gpsimd.tensor_scalar(out=d[:, hs], in0=d[:, hs], scalar1=0.0, scalar2=EPS_STD, op0=ALU.max, op1=ALU.add)
+                else:
+                    nc.vector.scalar_tensor_tensor(out=d[:, hs], in0=acc_g[h][:, 0:H], scalar=INV, in1=d[:, hs], op0=ALU.mult, op1=ALU.subtract)
+                    nc.vector.tensor_scalar(out=d[:, hs], in0=d[:, hs], scalar1=0.0, scalar2=EPS_STD, op0=ALU.max, op1=ALU.add)
 
-            def s4():
-                nc.scalar.activation(out=res[:, 3, hs], in_=msq[:, hs], func=ACT.Sqrt)
-                nc.vector.tensor_tensor(out=res[:, 2, hs], in0=res[:, 2, hs], in1=base[:, hs], op=ALU.add)
+            def std():
+                nc.scalar.activation(out=res[h][:, 3, :], in_=d[:, hs], func=ACT.Sqrt)
+                nc.sync.dma_start(out=o0[:, 3, hs], in_=res[h][:, 3, :])
+                cast("s", 3, h)
+                nc.sync.dma_start(out=o1[:, 3, hs], in_=o8[h][:, 3, :].bitcast(U8))
 
-            def s5():
-                nc.sync.dma_start(out=o0[:, 3, hs], in_=res[:, 3, hs])
-                cast("s", 3, hs)
-                nc.vector.tensor_tensor(out=res[:, 1, hs], in0=res[:, 1, hs], in1=base[:, hs], op=ALU.add)
+            def base_to_psum():
+                bp = pz.tile([P, H], F32, name="z", tag="z")
+                nc.tensor.matmul(out=bp[:], lhsT=ident[:], rhs=late["base"][:, hs], start=True, stop=True)
+                late["bp"] = bp
 
-            def s6():
-                nc.sync.dma_start(out=o1[:, 3, hs], in_=o8[:, 3, hs].bitcast(U8))
-                cast("s", 2, hs)
-                nc.vector.tensor_tensor(out=res[:, 0, hs], in0=mz[:, hs], in1=base[:, hs], op=ALU.add)
+            def add_base(s0, s1):
+                if h == 0:
+                    b_in = late["bp"][:]
+                else:
+                    b_in = late["base"][:, hs]
+                nc.vector.tensor_tensor(out=res[h][:, s0:s1, :], in0=b_in.unsqueeze(1).to_broadcast([P, s1 - s0, H]), in1=res[h][:, s0:s1, :], op=ALU.add)
+                nc.sync.dma_start(out=o0[:, s0:s1, hs], in_=res[h][:, s0:s1, :])
 
-            def s7():
-                nc.sync.dma_start(out=o0[:, 0:3, hs], in_=res[:, 0:3, hs])
-                cast("s" if h == 0 else "v", 1, hs)
-                cast("s", 0, hs)
+            def casts(s0, s1, engs):
+                for s in range(s0, s1):
+                    cast(engs[s - s0], s, h)
+                nc.sync.dma_start(out=o1[:, s0:s1, hs], in_=o8[h][:, s0:s1, :].bitcast(U8))
 
-            def s8():
-                nc.sync.dma_start(out=o1[:, 0:3, hs], in_=o8[:, 0:3, hs].bitcast(U8))
-
-            return [s1, s2, s3, s4, s5, s6, s7, s8]
+            return {"mean_t": mean_t, "mean_vg": mean_vg, "mean_sq": mean_sq, "var": var, "std": std, "base_to_psum": base_to_psum, "add_base": add_base, "casts": casts}
 
         nc.sync.dma_start(out=x_sb[:], in_=x_rows)
         load_e(0)
@@ -310,6 +320,9 @@ def tile_gnnlayer_pa_kernel(tc, x, e_enc, W_pre, b_pre, out_0, out_1):
         quant_w(1, 0, 1, 2)
         transposes(1, head=True)
         copy_out(1)
+        replicate_x(XR0, XR1)
+        quant(0, 2, 4)
+        replicate_x(XR1, NJ)
         load_e(3)
         load_e(4)
         load_w(2, 0, 1)
@@ -320,15 +333,15 @@ def tile_gnnlayer_pa_kernel(tc, x, e_enc, W_pre, b_pre, out_0, out_1):
         for n in range(5, NJ, 2):
             if (n + 7) // 2 < NPR:
                 tr_after[n] = (n + 7) // 2
-        loads_after = {0: [("e", 5)], 1: [("e", 6), ("w", 1, 0, 1), ("w", 1, 1, 1)], 2: [("e", 7)], 3: [("e", 8)], 9: [("w", 0, 0, 0), ("w", 0, 1, 0)], 17: [("w", 0, 0, 1), ("w", 0, 1, 1)]}
+        loads_after = {0: [("e", 5)], 1: [("e", 6), ("w", 1, 0, 1), ("w", 1, 1, 1)], 2: [("e", 7)], 3: [("e", 8)], 7: [("w", 0, 0, 0)], 11: [("w", 0, 1, 0)], 15: [("w", 0, 0, 1)], 19: [("w", 0, 1, 1)]}
         for n in range(5, NJ, 2):
             if (n + 7) // 2 + 3 < NPR:
                 loads_after.setdefault(n, []).append(("e", (n + 7) // 2 + 3))
-        v_after = {0: [("qe", 0, 2, 4)], 1: [("xr", XR0, XR1)], 3: [("qe", 1, 0, 4)], 4: [("qe", 2, 0, 4)], 6: [("xr", XR1, NJ)]}
+        v_after = {2: [("qe", 1, 0, 4)], 4: [("qe", 2, 0, 4)]}
         for q in range(3, 8):
             v_after.setdefault(4 * q - 4, []).append(("qe", q, 0, 4))
         for i in range(3):
-            v_after.setdefault(8 * i + 11, []).append(("qw",) + (w_later[2 * i][0], w_later[2 * i][2]))
+            v_after.setdefault(8 * i + 12, []).append(("qw",) + (w_later[2 * i][0], w_later[2 * i][2]))
 
         def il_piece(n):
             w, g, h = w_later[n // 2]
@@ -355,22 +368,42 @@ def tile_gnnlayer_pa_kernel(tc, x, e_enc, W_pre, b_pre, out_0, out_1):
                     load_w(a[1], a[2], a[3])
             if j == 4:
                 nc.sync.dma_start(out=b_bc[:], in_=b_pre.partition_broadcast(P))
-            if j == 21:
-                small_products()
+            if j == 22:
+                source_sum_a()
+            if j == 24:
+                source_sum_b()
 
         sig[1] = ptp.tile([P, H], F32, name="tp", tag="tp")
         late["mm"] = shr.tile([P, 2, F], F32, name="mm", tag="sha", align_bytes=64)
-        steps = []
+        f0 = finish_steps(0)
+        f1 = finish_steps(1)
         for j in range(NJ):
             bank(j, 1)
             if j in (0, 2):
                 il_piece(14 + j // 2)
-            if j == 3:
-                quant_w(0, 1, 0, 2)
             if j == 4:
-                target_term()
-                steps = finish_steps(0)
-            if j >= 6 and steps:
-                steps.pop(0)()
-        for s in finish_steps(1):
-            s()
+                quant_w(0, 1, 0, 2)
+                f0["mean_t"]()
+                f0["mean_vg"]()
+            if j == 6:
+                f0["mean_sq"]()
+            if j in (7, 8):
+                target_term(j - 7)
+            if j == 8:
+                f0["var"]()
+            if j == 10:
+                f0["base_to_psum"]()
+            if j == 12:
+                f0["std"]()
+                f0["add_base"](0, 3)
+            if j == 14:
+                f0["casts"](0, 3, "sss")
+        f1["mean_t"]()
+        f1["mean_vg"]()
+        f1["mean_sq"]()
+        f1["add_base"](1, 3)
+        f1["var"]()
+        f1["casts"](1, 3, "ss")
+        f1["std"]()
+        f1["add_base"](0, 1)
+        f1["casts"](0, 1, "v")

@@ -172,12 +172,19 @@ def tile_gnnlayer_pa_kernel(tc, x, e_enc, W_pre, b_pre, out_0, out_1):
             a_t, b_v, c_g = SPLIT[h]
             hs = slice(H * h, H * (h + 1))
             z = pz.tile([P, H], F32, name="z", tag="z")
+
+            def sum_passes():
+                for g in range(2):
+                    mx(sig[h][:, 0:a_t], ec[:, j, 128 * g : 128 * (g + 1)], es[:, j, 128 * g : 128 * (g + 1)], 2, h, g, a_t, j == 0 and g == 0, j == NJ - 1 and g == 1)
+
+            if j == NJ - 1:
+                sum_passes()
             for g in range(2):
                 mx(z[:], ec[:, j, 128 * g : 128 * (g + 1)], es[:, j, 128 * g : 128 * (g + 1)], 2, h, g, H, g == 0, False)
             for g in range(2):
                 mx(z[:], xrep_c[:, j, g, :], xrep_s[:, j, g, :], 1, h, g, H, False, g == 1)
-            for g in range(2):
-                mx(sig[h][:, 0:a_t], ec[:, j, 128 * g : 128 * (g + 1)], es[:, j, 128 * g : 128 * (g + 1)], 2, h, g, a_t, j == 0 and g == 0, j == NJ - 1 and g == 1)
+            if j < NJ - 1:
+                sum_passes()
             if j == 0:
                 dst = acc_g[h]
             else:
@@ -241,16 +248,10 @@ def tile_gnnlayer_pa_kernel(tc, x, e_enc, W_pre, b_pre, out_0, out_1):
 
             def mean_sq():
                 nc.scalar.activation(out=d[:, hs], in_=res[h][:, 0, :], func=ACT.Square)
-                if h == 0:
-                    nc.scalar.activation(out=q[:, hs], in_=acc_g[h][:, 0:H], func=ACT.Copy, scale=INV)
 
             def var():
-                if h == 0:
-                    nc.gpsimd.tensor_tensor(out=d[:, hs], in0=q[:, hs], in1=d[:, hs], op=ALU.subtract)
-                    nc.gpsimd.tensor_scalar(out=d[:, hs], in0=d[:, hs], scalar1=0.0, scalar2=EPS_STD, op0=ALU.max, op1=ALU.add)
-                else:
-                    nc.vector.scalar_tensor_tensor(out=d[:, hs], in0=acc_g[h][:, 0:H], scalar=INV, in1=d[:, hs], op0=ALU.mult, op1=ALU.subtract)
-                    nc.vector.tensor_scalar(out=d[:, hs], in0=d[:, hs], scalar1=0.0, scalar2=EPS_STD, op0=ALU.max, op1=ALU.add)
+                nc.vector.scalar_tensor_tensor(out=d[:, hs], in0=acc_g[h][:, 0:H], scalar=INV, in1=d[:, hs], op0=ALU.mult, op1=ALU.subtract)
+                nc.vector.tensor_scalar(out=d[:, hs], in0=d[:, hs], scalar1=0.0, scalar2=EPS_STD, op0=ALU.max, op1=ALU.add)
 
             def std():
                 nc.scalar.activation(out=res[h][:, 3, :], in_=d[:, hs], func=ACT.Sqrt)
@@ -264,10 +265,7 @@ def tile_gnnlayer_pa_kernel(tc, x, e_enc, W_pre, b_pre, out_0, out_1):
                 late["bp"] = bp
 
             def add_base(s0, s1):
-                if h == 0:
-                    b_in = late["bp"][:]
-                else:
-                    b_in = late["base"][:, hs]
+                b_in = late["base"][:, hs]
                 nc.vector.tensor_tensor(out=res[h][:, s0:s1, :], in0=b_in.unsqueeze(1).to_broadcast([P, s1 - s0, H]), in1=res[h][:, s0:s1, :], op=ALU.add)
                 nc.sync.dma_start(out=o0[:, s0:s1, hs], in_=res[h][:, s0:s1, :])
 
@@ -391,8 +389,6 @@ def tile_gnnlayer_pa_kernel(tc, x, e_enc, W_pre, b_pre, out_0, out_1):
                 target_term(j - 7)
             if j == 8:
                 f0["var"]()
-            if j == 10:
-                f0["base_to_psum"]()
             if j == 12:
                 f0["std"]()
                 f0["add_base"](0, 3)

@@ -19,11 +19,12 @@ NJ = 32
 NPR = 16
 F = 1024
 H = 512
-SPLIT = ((256, 192, 64), (256, 192, 64))
+SPLIT = ((256, 224, 32), (256, 256, 0))
 FS = 256
 XR0 = 4
 XR1 = 12
-MANUAL = False
+MANUAL = True
+ST2 = 3
 Y_SCALE = 160.0
 EPS_STD = 1e-5
 INV = 1.0 / 32.0
@@ -39,14 +40,12 @@ def tile_gnnlayer_pa_kernel(tc, x, e_enc, W_pre, b_pre, out_0, out_1):
     sig_w = SPLIT[0][0] + SPLIT[1][0]
 
     with ExitStack() as ctx:
-        if MANUAL:
-            ctx.enter_context(tc.manual_schedule())
         const = ctx.enter_context(tc.tile_pool(name="const", bufs=1))
         wraw_pool = ctx.enter_context(tc.tile_pool(name="wraw", bufs=4))
         wgrp_pool = ctx.enter_context(tc.tile_pool(name="wgrp", bufs=2))
         eraw_pool = ctx.enter_context(tc.tile_pool(name="eraw", bufs=3))
         egrp_pool = ctx.enter_context(tc.tile_pool(name="egrp", bufs=2))
-        st_pool = ctx.enter_context(tc.tile_pool(name="st", bufs=4))
+        st2_pool = ctx.enter_context(tc.tile_pool(name="st2", bufs=ST2))
         shr = ctx.enter_context(tc.tile_pool(name="shr", bufs=1))
         ptp = ctx.enter_context(tc.psum_pool(name="ptp", bufs=2))
         pz = ctx.enter_context(tc.psum_pool(name="pz", bufs=5))
@@ -59,9 +58,11 @@ def tile_gnnlayer_pa_kernel(tc, x, e_enc, W_pre, b_pre, out_0, out_1):
         make_identity(nc, ident[:])
         bd = const.tile([P, P], F32, name="bd")
         make_block_diagonal(nc, bd[:], 32)
+        if MANUAL:
+            ctx.enter_context(tc.manual_schedule())
 
-        x_sb = const.tile([P, 1024], BF16, name="x_sb")
-        xg = const.tile([P, 1024], BF16, name="xg", align_bytes=64)
+        x_sb = shr.tile([P, 1024], BF16, name="x_sb", tag="shc", align_bytes=64)
+        xg = shr.tile([P, 1024], BF16, name="xg", tag="shd", align_bytes=64)
         xg4 = shr.tile([P, 4096], BF16, name="xg4", tag="sha", align_bytes=64)
         xc = const.tile([P, 256], I32, name="xc", align_bytes=64)
         xs = const.tile([P, 256], U8, name="xs", align_bytes=64)
@@ -75,10 +76,8 @@ def tile_gnnlayer_pa_kernel(tc, x, e_enc, W_pre, b_pre, out_0, out_1):
         es = const.tile([P, NJ, 256], U8, name="es", align_bytes=64)
         b_bc = const.tile([P, F], BF16, name="b_bc")
         late = {}
-        s_sb = const.tile([P, sig_w], F32, name="s_sb")
-        srep32 = const.tile([P, sig_w], F32, name="srep32")
         res = [const.tile([P, 4, H], F32, name="res%d" % h) for h in range(2)]
-        acc_g = [const.tile([P, H + SPLIT[h][2]], F32, name="acc_g%d" % h) for h in range(2)]
+        acc_g = [const.tile([P, 1 + h, H + SPLIT[h][2]], F32, name="acc_g%d" % h) for h in range(2)]
         acc_v = [const.tile([P, SPLIT[h][1]], F32, name="acc_v%d" % h) for h in range(2)]
         o8 = [const.tile([P, 4, H], FP8, name="o8%d" % h) for h in range(2)]
         sig = {0: psig.tile([P, H], F32, name="sig")}
@@ -116,8 +115,10 @@ def tile_gnnlayer_pa_kernel(tc, x, e_enc, W_pre, b_pre, out_0, out_1):
             src = wraw[(w, g, h)][:, :, f0:f1].rearrange("p t f -> p f t")
             if eng == "v":
                 nc.vector.tensor_copy(out=dst, in_=src)
-            else:
+            elif eng == "s":
                 nc.scalar.copy(out=dst, in_=src)
+            else:
+                nc.gpsimd.tensor_scalar(out=dst, in0=src, scalar1=1.0, scalar2=0.0, op0=ALU.mult, op1=ALU.add)
 
         def quant_w(w, h, g0, g1):
             nc.vector.quantize_mx(
@@ -185,10 +186,12 @@ def tile_gnnlayer_pa_kernel(tc, x, e_enc, W_pre, b_pre, out_0, out_1):
                 mx(z[:], xrep_c[:, j, g, :], xrep_s[:, j, g, :], 1, h, g, H, False, g == 1)
             if j < NJ - 1:
                 sum_passes()
-            if j == 0:
-                dst = acc_g[h]
+            if j <= h:
+                dst = acc_g[h][:, j, :]
             else:
-                dst = st_pool.tile([P, H + c_g], F32, name="st", tag="st")
+                if j % 2 == 0 or j == 1:
+                    late["st2"] = st2_pool.tile([P, 2, H + c_g], F32, name="st2", tag="st2")
+                dst = late["st2"][:, j % 2, :]
             nc.scalar.activation(out=dst[:, 0:H], in_=z[:], func=ACT.Square)
             if c_g:
                 nc.scalar.copy(out=dst[:, H : H + c_g], in_=z[:, H - c_g : H])
@@ -200,20 +203,29 @@ def tile_gnnlayer_pa_kernel(tc, x, e_enc, W_pre, b_pre, out_0, out_1):
                 nc.vector.tensor_tensor(out=res[h][:, 2, :], in0=z[:], in1=res[h][:, 2, :], op=ALU.max)
                 nc.vector.tensor_tensor(out=res[h][:, 1, :], in0=z[:], in1=res[h][:, 1, :], op=ALU.min)
                 nc.vector.tensor_tensor(out=acc_v[h][:], in0=z[:, a_t : a_t + b_v], in1=acc_v[h][:], op=ALU.add)
-                add = nc.vector.tensor_tensor if (h == 1 and j == NJ - 1) else nc.gpsimd.tensor_tensor
-                add(out=acc_g[h][:], in0=acc_g[h][:], in1=dst[:], op=ALU.add)
+                if h == 0:
+                    nc.gpsimd.tensor_tensor(out=acc_g[0][:, 0, :], in0=acc_g[0][:, 0, :], in1=dst, op=ALU.add)
+                elif j >= NJ - 2:
+                    add = nc.vector.tensor_tensor if j == NJ - 1 else nc.gpsimd.tensor_tensor
+                    add(out=acc_g[1][:, 0, :], in0=acc_g[1][:, 0, :], in1=dst, op=ALU.add)
+                elif j % 2 == 1 and j > 1:
+                    nc.gpsimd.tensor_tensor(out=acc_g[1][:], in0=acc_g[1][:], in1=late["st2"][:], op=ALU.add)
+                    if j == NJ - 3:
+                        nc.gpsimd.tensor_tensor(out=acc_g[1][:, 0, :], in0=acc_g[1][:, 0, :], in1=acc_g[1][:, 1, :], op=ALU.add)
 
         def source_sum_a():
+            late["s_sb"] = shr.tile([P, sig_w], F32, name="s_sb", tag="shc", align_bytes=64)
+            late["srep32"] = shr.tile([P, sig_w], F32, name="srep32", tag="shd", align_bytes=64)
             s_ps = pz.tile([P, H], F32, name="z", tag="z")
             for h in range(2):
                 for g in range(2):
                     mx(s_ps[:, sig_off[h] : sig_off[h] + SPLIT[h][0]], xc[:, 128 * g : 128 * (g + 1)], xs[:, 128 * g : 128 * (g + 1)], 1, h, g, SPLIT[h][0], g == 0, g == 1)
-            nc.scalar.copy(out=s_sb[:], in_=s_ps[:, 0:sig_w])
+            nc.scalar.copy(out=late["s_sb"][:], in_=s_ps[:, 0:sig_w])
 
         def source_sum_b():
             srep_ps = pz.tile([P, H], F32, name="z", tag="z")
-            nc.tensor.matmul(out=srep_ps[:, 0:sig_w], lhsT=bd[:], rhs=s_sb[:], start=True, stop=True)
-            nc.scalar.activation(out=srep32[:], in_=srep_ps[:, 0:sig_w], func=ACT.Copy, scale=INV)
+            nc.tensor.matmul(out=srep_ps[:, 0:sig_w], lhsT=bd[:], rhs=late["s_sb"][:], start=True, stop=True)
+            nc.scalar.activation(out=late["srep32"][:], in_=srep_ps[:, 0:sig_w], func=ACT.Copy, scale=INV)
 
         def target_term(h):
             if "base" not in late:
@@ -238,20 +250,26 @@ def tile_gnnlayer_pa_kernel(tc, x, e_enc, W_pre, b_pre, out_0, out_1):
 
             def mean_t():
                 nc.vector.scalar_tensor_tensor(
-                    out=res[h][:, 0, 0:a_t], in0=sig[h][:, 0:a_t], scalar=INV, in1=srep32[:, sig_off[h] : sig_off[h] + a_t], op0=ALU.mult, op1=ALU.add
+                    out=res[h][:, 0, 0:a_t], in0=sig[h][:, 0:a_t], scalar=INV, in1=late["srep32"][:, sig_off[h] : sig_off[h] + a_t], op0=ALU.mult, op1=ALU.add
                 )
 
             def mean_vg():
                 nc.scalar.activation(out=res[h][:, 0, a_t : a_t + b_v], in_=acc_v[h][:], func=ACT.Copy, scale=INV)
                 if c_g:
-                    nc.scalar.activation(out=res[h][:, 0, H - c_g : H], in_=acc_g[h][:, H : H + c_g], func=ACT.Copy, scale=INV)
+                    nc.scalar.activation(out=res[h][:, 0, H - c_g : H], in_=acc_g[h][:, 0, H : H + c_g], func=ACT.Copy, scale=INV)
 
             def mean_sq():
                 nc.scalar.activation(out=d[:, hs], in_=res[h][:, 0, :], func=ACT.Square)
+                if h == 0:
+                    nc.scalar.activation(out=q[:, hs], in_=acc_g[h][:, 0, 0:H], func=ACT.Copy, scale=INV)
 
             def var():
-                nc.vector.scalar_tensor_tensor(out=d[:, hs], in0=acc_g[h][:, 0:H], scalar=INV, in1=d[:, hs], op0=ALU.mult, op1=ALU.subtract)
-                nc.vector.tensor_scalar(out=d[:, hs], in0=d[:, hs], scalar1=0.0, scalar2=EPS_STD, op0=ALU.max, op1=ALU.add)
+                if h == 0:
+                    nc.gpsimd.tensor_tensor(out=d[:, hs], in0=q[:, hs], in1=d[:, hs], op=ALU.subtract)
+                    nc.gpsimd.tensor_scalar(out=d[:, hs], in0=d[:, hs], scalar1=0.0, scalar2=EPS_STD, op0=ALU.max, op1=ALU.add)
+                else:
+                    nc.vector.scalar_tensor_tensor(out=d[:, hs], in0=acc_g[h][:, 0, 0:H], scalar=INV, in1=d[:, hs], op0=ALU.mult, op1=ALU.subtract)
+                    nc.vector.tensor_scalar(out=d[:, hs], in0=d[:, hs], scalar1=0.0, scalar2=EPS_STD, op0=ALU.max, op1=ALU.add)
 
             def std():
                 nc.scalar.activation(out=res[h][:, 3, :], in_=d[:, hs], func=ACT.Sqrt)
@@ -265,7 +283,7 @@ def tile_gnnlayer_pa_kernel(tc, x, e_enc, W_pre, b_pre, out_0, out_1):
                 late["bp"] = bp
 
             def add_base(s0, s1):
-                b_in = late["base"][:, hs]
+                b_in = late["bp"][:] if h == 0 else late["base"][:, hs]
                 nc.vector.tensor_tensor(out=res[h][:, s0:s1, :], in0=b_in.unsqueeze(1).to_broadcast([P, s1 - s0, H]), in1=res[h][:, s0:s1, :], op=ALU.add)
                 nc.sync.dma_start(out=o0[:, s0:s1, hs], in_=res[h][:, s0:s1, :])
 
@@ -327,28 +345,31 @@ def tile_gnnlayer_pa_kernel(tc, x, e_enc, W_pre, b_pre, out_0, out_1):
         load_w(2, 1, 1)
 
         w_later = [(2, 0, 1), (2, 1, 1), (1, 0, 1), (1, 1, 1), (0, 0, 0), (0, 1, 0), (0, 0, 1), (0, 1, 1)]
+        g_pieces = {14: 12, 17: 13, 20: 14, 23: 15}
         tr_after = {0: 2, 1: 3, 2: 4, 3: 5}
         for n in range(5, NJ, 2):
             if (n + 7) // 2 < NPR:
                 tr_after[n] = (n + 7) // 2
-        loads_after = {0: [("e", 5)], 1: [("e", 6), ("w", 1, 0, 1), ("w", 1, 1, 1)], 2: [("e", 7)], 3: [("e", 8)], 7: [("w", 0, 0, 0)], 11: [("w", 0, 1, 0)], 15: [("w", 0, 0, 1)], 19: [("w", 0, 1, 1)]}
+        loads_after = {0: [("e", 5)], 1: [("e", 6), ("w", 1, 0, 1), ("w", 1, 1, 1)], 2: [("e", 7)], 3: [("e", 8)], 7: [("w", 0, 0, 1)], 11: [("w", 0, 1, 1)], 15: [("w", 0, 0, 0)], 19: [("w", 0, 1, 0)]}
         for n in range(5, NJ, 2):
             if (n + 7) // 2 + 3 < NPR:
                 loads_after.setdefault(n, []).append(("e", (n + 7) // 2 + 3))
         v_after = {2: [("qe", 1, 0, 4)], 4: [("qe", 2, 0, 4)]}
         for q in range(3, 8):
             v_after.setdefault(4 * q - 4, []).append(("qe", q, 0, 4))
-        for i in range(3):
-            v_after.setdefault(8 * i + 12, []).append(("qw",) + (w_later[2 * i][0], w_later[2 * i][2]))
+        for n, w, h in ((12, 2, 1), (19, 1, 1), (25, 0, 1), (28, 0, 0)):
+            v_after.setdefault(n, []).append(("qw", w, h))
 
-        def il_piece(n):
+        def il_piece(n, eng="s"):
             w, g, h = w_later[n // 2]
-            interleave_w(w, g, h, "s", 256 * (n % 2), 256 * (n % 2 + 1))
+            interleave_w(w, g, h, eng, 256 * (n % 2), 256 * (n % 2 + 1))
 
         for j in range(NJ):
             bank(j, 0)
-            if j % 2 == 0 and j >= 4:
+            if j % 2 == 0 and 4 <= j <= 26:
                 il_piece(j // 2 - 2)
+            if j in g_pieces:
+                il_piece(g_pieces[j], "g")
             for a in v_after.get(j, []):
                 if a[0] == "qe":
                     quant(a[1], a[2], a[3])
@@ -377,22 +398,20 @@ def tile_gnnlayer_pa_kernel(tc, x, e_enc, W_pre, b_pre, out_0, out_1):
         f1 = finish_steps(1)
         for j in range(NJ):
             bank(j, 1)
-            if j in (0, 2):
-                il_piece(14 + j // 2)
-            if j == 4:
-                quant_w(0, 1, 0, 2)
+            if j in (0, 1):
+                target_term(j)
+            if j == 2:
                 f0["mean_t"]()
                 f0["mean_vg"]()
-            if j == 6:
+            if j == 4:
                 f0["mean_sq"]()
-            if j in (7, 8):
-                target_term(j - 7)
-            if j == 8:
+                f0["base_to_psum"]()
+            if j == 6:
                 f0["var"]()
-            if j == 12:
-                f0["std"]()
                 f0["add_base"](0, 3)
-            if j == 14:
+            if j == 9:
+                f0["std"]()
+            if j == 11:
                 f0["casts"](0, 3, "sss")
         f1["mean_t"]()
         f1["mean_vg"]()

@@ -111,8 +111,8 @@ def tile_gnnlayer_pa_kernel(tc, x, e_enc, W_pre, b_pre, out_0, out_1):
         def interleave_w(w, g, h, eng, f0=0, f1=H):
             if (w, h) not in wgrp:
                 wgrp[(w, h)] = wgrp_pool.tile([P, 2, 2048], BF16, name="wgrp", tag="wgrp", align_bytes=64)
-            dst = wgrp[(w, h)][:, g, 4 * f0 : 4 * f1].rearrange("p (f t) -> p f t", t=4)
-            src = wraw[(w, g, h)][:, :, f0:f1].rearrange("p t f -> p f t")
+            dst = wgrp[(w, h)][:, g, 4 * f0 : 4 * f1].rearrange("p (c i t) -> p c t i", i=4, t=4)
+            src = wraw[(w, g, h)][:, :, f0:f1].rearrange("p t (c i) -> p c t i", i=4)
             if eng == "v":
                 nc.vector.tensor_copy(out=dst, in_=src)
             elif eng == "s":

@@ -24,6 +24,7 @@ FS = 256
 XR0 = 4
 XR1 = 12
 MANUAL = True
+SINGLE = 26
 ST2 = 3
 Y_SCALE = 160.0
 EPS_STD = 1e-5
@@ -205,12 +206,12 @@ def tile_gnnlayer_pa_kernel(tc, x, e_enc, W_pre, b_pre, out_0, out_1):
                 nc.vector.tensor_tensor(out=acc_v[h][:], in0=z[:, a_t : a_t + b_v], in1=acc_v[h][:], op=ALU.add)
                 if h == 0:
                     nc.gpsimd.tensor_tensor(out=acc_g[0][:, 0, :], in0=acc_g[0][:, 0, :], in1=dst, op=ALU.add)
-                elif j >= NJ - 2:
+                elif j >= SINGLE:
                     add = nc.vector.tensor_tensor if j == NJ - 1 else nc.gpsimd.tensor_tensor
                     add(out=acc_g[1][:, 0, :], in0=acc_g[1][:, 0, :], in1=dst, op=ALU.add)
                 elif j % 2 == 1 and j > 1:
                     nc.gpsimd.tensor_tensor(out=acc_g[1][:], in0=acc_g[1][:], in1=late["st2"][:], op=ALU.add)
-                    if j == NJ - 3:
+                    if j == SINGLE - 1:
                         nc.gpsimd.tensor_tensor(out=acc_g[1][:, 0, :], in0=acc_g[1][:, 0, :], in1=acc_g[1][:, 1, :], op=ALU.add)
 
         def source_sum_a():
@@ -345,19 +346,20 @@ def tile_gnnlayer_pa_kernel(tc, x, e_enc, W_pre, b_pre, out_0, out_1):
         load_w(2, 1, 1)
 
         w_later = [(2, 0, 1), (2, 1, 1), (1, 0, 1), (1, 1, 1), (0, 0, 0), (0, 1, 0), (0, 0, 1), (0, 1, 1)]
-        g_pieces = {14: 12, 17: 13, 20: 14, 23: 15}
+        g_pieces = {}
+        s_late = {27: 12, 28: 13, 29: 14, 30: 15}
         tr_after = {0: 2, 1: 3, 2: 4, 3: 5}
         for n in range(5, NJ, 2):
             if (n + 7) // 2 < NPR:
                 tr_after[n] = (n + 7) // 2
-        loads_after = {0: [("e", 5)], 1: [("e", 6), ("w", 1, 0, 1), ("w", 1, 1, 1)], 2: [("e", 7)], 3: [("e", 8)], 7: [("w", 0, 0, 1)], 11: [("w", 0, 1, 1)], 15: [("w", 0, 0, 0)], 19: [("w", 0, 1, 0)]}
+        loads_after = {0: [("e", 5)], 1: [("e", 6), ("w", 1, 0, 1), ("w", 1, 1, 1)], 2: [("e", 7)], 3: [("e", 8)], 7: [("w", 0, 0, 0)], 11: [("w", 0, 1, 0)], 15: [("w", 0, 0, 1)], 19: [("w", 0, 1, 1)]}
         for n in range(5, NJ, 2):
             if (n + 7) // 2 + 3 < NPR:
                 loads_after.setdefault(n, []).append(("e", (n + 7) // 2 + 3))
         v_after = {2: [("qe", 1, 0, 4)], 4: [("qe", 2, 0, 4)]}
         for q in range(3, 8):
             v_after.setdefault(4 * q - 4, []).append(("qe", q, 0, 4))
-        for n, w, h in ((12, 2, 1), (19, 1, 1), (25, 0, 1), (28, 0, 0)):
+        for n, w, h in ((11, 2, 1), (19, 1, 1), (27, 0, 0), (31, 0, 1)):
             v_after.setdefault(n, []).append(("qw", w, h))
 
         def il_piece(n, eng="s"):
@@ -368,8 +370,8 @@ def tile_gnnlayer_pa_kernel(tc, x, e_enc, W_pre, b_pre, out_0, out_1):
             bank(j, 0)
             if j % 2 == 0 and 4 <= j <= 26:
                 il_piece(j // 2 - 2)
-            if j in g_pieces:
-                il_piece(g_pieces[j], "g")
+            if j in s_late:
+                il_piece(s_late[j])
             for a in v_after.get(j, []):
                 if a[0] == "qe":
                     quant(a[1], a[2], a[3])

@@ -19,12 +19,12 @@ NJ = 32
 NPR = 16
 F = 1024
 H = 512
-SPLIT = ((256, 224, 32), (256, 256, 0))
+SPLIT = ((256, 256, 0), (256, 256, 0))
 FS = 256
 XR0 = 4
 XR1 = 12
 MANUAL = True
-SINGLE = 26
+SINGLE = 30
 ST2 = 3
 Y_SCALE = 160.0
 EPS_STD = 1e-5
@@ -402,14 +402,16 @@ def tile_gnnlayer_pa_kernel(tc, x, e_enc, W_pre, b_pre, out_0, out_1):
             bank(j, 1)
             if j in (0, 1):
                 target_term(j)
-            if j == 2:
+            if j == 1:
                 f0["mean_t"]()
                 f0["mean_vg"]()
-            if j == 4:
+            if j == 2:
                 f0["mean_sq"]()
+            if j == 2:
+                f0["var"]()
+            if j == 4:
                 f0["base_to_psum"]()
             if j == 6:
-                f0["var"]()
                 f0["add_base"](0, 3)
             if j == 9:
                 f0["std"]()

@@ -170,7 +170,7 @@ def tile_gnnlayer_pa_kernel(tc, x, e_enc, W_pre, b_pre, out_0, out_1):
                 stop=stop,
             )
 
-        def bank(j, h):
+        def bank(j, h, before_vector=None):
             a_t, b_v, c_g = SPLIT[h]
             hs = slice(H * h, H * (h + 1))
             z = pz.tile([P, H], F32, name="z", tag="z")
@@ -201,6 +201,8 @@ def tile_gnnlayer_pa_kernel(tc, x, e_enc, W_pre, b_pre, out_0, out_1):
                 nc.scalar.copy(out=res[h][:, 1, :], in_=z[:])
                 nc.vector.tensor_copy(out=acc_v[h][:], in_=z[:, a_t : a_t + b_v])
             else:
+                if before_vector:
+                    before_vector()
                 nc.vector.tensor_tensor(out=res[h][:, 2, :], in0=z[:], in1=res[h][:, 2, :], op=ALU.max)
                 nc.vector.tensor_tensor(out=res[h][:, 1, :], in0=z[:], in1=res[h][:, 1, :], op=ALU.min)
                 nc.vector.tensor_tensor(out=acc_v[h][:], in0=z[:, a_t : a_t + b_v], in1=acc_v[h][:], op=ALU.add)
@@ -366,8 +368,10 @@ def tile_gnnlayer_pa_kernel(tc, x, e_enc, W_pre, b_pre, out_0, out_1):
             w, g, h = w_later[n // 2]
             interleave_w(w, g, h, eng, 256 * (n % 2), 256 * (n % 2 + 1))
 
+        late["mm"] = shr.tile([P, 2, F], F32, name="mm", tag="sha", align_bytes=64)
+        f0 = finish_steps(0)
         for j in range(NJ):
-            bank(j, 0)
+            bank(j, 0, f0["mean_t"] if j == NJ - 1 else None)
             if j % 2 == 0 and 4 <= j <= 26:
                 il_piece(j // 2 - 2)
             if j in s_late:
@@ -395,29 +399,25 @@ def tile_gnnlayer_pa_kernel(tc, x, e_enc, W_pre, b_pre, out_0, out_1):
                 source_sum_b()
 
         sig[1] = ptp.tile([P, H], F32, name="tp", tag="tp")
-        late["mm"] = shr.tile([P, 2, F], F32, name="mm", tag="sha", align_bytes=64)
-        f0 = finish_steps(0)
         f1 = finish_steps(1)
         for j in range(NJ):
-            bank(j, 1)
-            if j in (0, 1):
-                target_term(j)
-            if j == 1:
-                f0["mean_t"]()
+            bank(j, 1, f1["mean_t"] if j == NJ - 1 else None)
+            if j in (2, 3):
+                target_term(0 if j == 2 else 1)
+            if j == 0:
                 f0["mean_vg"]()
-            if j == 2:
+            if j == 1:
                 f0["mean_sq"]()
-            if j == 2:
+            if j == 1:
                 f0["var"]()
-            if j == 4:
+            if j == 5:
                 f0["base_to_psum"]()
-            if j == 6:
+            if j == 7:
                 f0["add_base"](0, 3)
             if j == 9:
                 f0["std"]()
             if j == 11:
                 f0["casts"](0, 3, "sss")
-        f1["mean_t"]()
         f1["mean_vg"]()
         f1["mean_sq"]()
         f1["add_base"](1, 3)

@@ -48,7 +48,7 @@ def tile_gnnlayer_pa_kernel(tc, x, e_enc, W_pre, b_pre, out_0, out_1):
         egrp_pool = ctx.enter_context(tc.tile_pool(name="egrp", bufs=2))
         st2_pool = ctx.enter_context(tc.tile_pool(name="st2", bufs=ST2))
         shr = ctx.enter_context(tc.tile_pool(name="shr", bufs=1))
-        ptp = ctx.enter_context(tc.psum_pool(name="ptp", bufs=2))
+        ptp = ctx.enter_context(tc.psum_pool(name="ptp", bufs=1))
         pz = ctx.enter_context(tc.psum_pool(name="pz", bufs=5))
         psig = ctx.enter_context(tc.psum_pool(name="psig", bufs=1))
 
@@ -64,10 +64,8 @@ def tile_gnnlayer_pa_kernel(tc, x, e_enc, W_pre, b_pre, out_0, out_1):
 
         x_sb = shr.tile([P, 1024], BF16, name="x_sb", tag="shc", align_bytes=64)
         xg = shr.tile([P, 1024], BF16, name="xg", tag="shd", align_bytes=64)
-        xg4 = shr.tile([P, 4096], BF16, name="xg4", tag="sha", align_bytes=64)
         xc = const.tile([P, 256], I32, name="xc", align_bytes=64)
         xs = const.tile([P, 256], U8, name="xs", align_bytes=64)
-        xc4 = shr.tile([P, 1024], I32, name="xc4", tag="shb", align_bytes=64)
         xs4 = const.tile([P, 1024], U8, name="xs4", align_bytes=64)
         xrep_c = const.tile([P, NJ, 2, P], I32, name="xrep_c", align_bytes=64)
         xrep_s = const.tile([P, NJ, 2, P], U8, name="xrep_s", align_bytes=64)
@@ -137,7 +135,7 @@ def tile_gnnlayer_pa_kernel(tc, x, e_enc, W_pre, b_pre, out_0, out_1):
                 if head:
                     tp = pz.tile([P, 4, P], F32, name="z", tag="z")
                 else:
-                    tp = ptp.tile([P, 4, P], F32, name="tp", tag="tp")
+                    tp = ptp.tile([P, 4, P], F32, name="tp%d" % jj, tag="tp%d" % jj)
                 words = raw[:, jj, :].bitcast(F32)
                 for g in range(2):
                     for u in range(2):
@@ -173,7 +171,12 @@ def tile_gnnlayer_pa_kernel(tc, x, e_enc, W_pre, b_pre, out_0, out_1):
         def bank(j, h, before_vector=None):
             a_t, b_v, c_g = SPLIT[h]
             hs = slice(H * h, H * (h + 1))
-            z = pz.tile([P, H], F32, name="z", tag="z")
+            if h == 1 and j % 7 == 6:
+                z = psig.tile([P, H], F32, name="sig")
+            elif h == 1 and j % 7 == 5:
+                z = ptp.tile([P, H], F32, name="tp1", tag="tp1")
+            else:
+                z = pz.tile([P, H], F32, name="z", tag="z")
 
             def sum_passes():
                 for g in range(2):
@@ -305,8 +308,8 @@ def tile_gnnlayer_pa_kernel(tc, x, e_enc, W_pre, b_pre, out_0, out_1):
         load_e(1)
         load_e(2)
 
-        nc.vector.memset(xs4[:].bitcast(I32), 0)
-        xt = ptp.tile([P, 4, P], F32, name="tp", tag="tp")
+        nc.vector.memset(xs[:].bitcast(I32), 0)
+        xt = ptp.tile([P, 4, P], F32, name="tp1", tag="tp1")
         xwords = x_sb[:].bitcast(F32)
         for g in range(2):
             for u in range(2):
@@ -318,11 +321,8 @@ def tile_gnnlayer_pa_kernel(tc, x, e_enc, W_pre, b_pre, out_0, out_1):
         transposes(0, head=True)
         copy_out(0)
         nc.vector.quantize_mx(out=xc[:].bitcast(FP8X4), scales=xs[:], in_=xg[:])
-        nc.vector.tensor_copy(
-            out=xg4[:].bitcast(F32).rearrange("p (c i u) -> p c i u", i=4, u=2),
-            in_=xg[:].bitcast(F32).rearrange("p (c u) -> p c u", u=2).unsqueeze(2).to_broadcast([P, 256, 4, 2]),
-        )
-        nc.vector.quantize_mx(out=xc4[:].bitcast(FP8X4), scales=xs4[:], in_=xg4[:])
+        for n in range(4):
+            nc.vector.tensor_copy(out=xs4[:].rearrange("p (c n) -> p c n", n=4)[:, :, n], in_=xs[:])
         interleave_w(2, 0, 0, "v", 0, FS)
         interleave_w(2, 0, 0, "s", FS, H)
         quant(0, 0, 2)
@@ -398,7 +398,7 @@ def tile_gnnlayer_pa_kernel(tc, x, e_enc, W_pre, b_pre, out_0, out_1):
             if j == 24:
                 source_sum_b()
 
-        sig[1] = ptp.tile([P, H], F32, name="tp", tag="tp")
+        sig[1] = ptp.tile([P, H], F32, name="tp0", tag="tp0")
         f1 = finish_steps(1)
         for j in range(NJ):
             bank(j, 1, f1["mean_t"] if j == NJ - 1 else None)

@@ -23,6 +23,7 @@ SPLIT = ((256, 256, 0), (256, 256, 0))
 FS = 256
 XR0 = 4
 XR1 = 12
+XA, XB, XR2 = 1, 3, 20
 MANUAL = True
 SINGLE = 30
 ST2 = 3
@@ -200,15 +201,16 @@ def tile_gnnlayer_pa_kernel(tc, x, e_enc, W_pre, b_pre, out_0, out_1):
             if c_g:
                 nc.scalar.copy(out=dst[:, H : H + c_g], in_=z[:, H - c_g : H])
             if j == 0:
-                nc.scalar.copy(out=res[h][:, 2, :], in_=z[:])
                 nc.scalar.copy(out=res[h][:, 1, :], in_=z[:])
-                nc.vector.tensor_copy(out=acc_v[h][:], in_=z[:, a_t : a_t + b_v])
             else:
                 if before_vector:
                     before_vector()
-                nc.vector.tensor_tensor(out=res[h][:, 2, :], in0=z[:], in1=res[h][:, 2, :], op=ALU.max)
+                if j == 1:
+                    nc.vector.tensor_tensor(out=acc_v[h][:], in0=z[:, a_t : a_t + b_v], in1=res[h][:, 1, a_t : a_t + b_v], op=ALU.add)
+                nc.vector.tensor_tensor(out=res[h][:, 2, :], in0=z[:], in1=res[h][:, 1 if j == 1 else 2, :], op=ALU.max)
                 nc.vector.tensor_tensor(out=res[h][:, 1, :], in0=z[:], in1=res[h][:, 1, :], op=ALU.min)
-                nc.vector.tensor_tensor(out=acc_v[h][:], in0=z[:, a_t : a_t + b_v], in1=acc_v[h][:], op=ALU.add)
+                if j > 1:
+                    nc.vector.tensor_tensor(out=acc_v[h][:], in0=z[:, a_t : a_t + b_v], in1=acc_v[h][:], op=ALU.add)
                 if h == 0:
                     nc.gpsimd.tensor_tensor(out=acc_g[0][:, 0, :], in0=acc_g[0][:, 0, :], in1=dst, op=ALU.add)
                 elif j >= SINGLE:
@@ -339,9 +341,8 @@ def tile_gnnlayer_pa_kernel(tc, x, e_enc, W_pre, b_pre, out_0, out_1):
         quant_w(1, 0, 1, 2)
         transposes(1, head=True)
         copy_out(1)
-        replicate_x(XR0, XR1)
         quant(0, 2, 4)
-        replicate_x(XR1, NJ)
+        replicate_x(XR0, XR1)
         load_e(3)
         load_e(4)
         load_w(2, 0, 1)
@@ -358,7 +359,10 @@ def tile_gnnlayer_pa_kernel(tc, x, e_enc, W_pre, b_pre, out_0, out_1):
         for n in range(5, NJ, 2):
             if (n + 7) // 2 + 3 < NPR:
                 loads_after.setdefault(n, []).append(("e", (n + 7) // 2 + 3))
-        v_after = {2: [("qe", 1, 0, 4)], 4: [("qe", 2, 0, 4)]}
+        v_after = {XA: [("xr", XR1, XR2)]}
+        v_after.setdefault(XB, []).append(("xr", XR2, NJ))
+        v_after.setdefault(2, []).append(("qe", 1, 0, 4))
+        v_after.setdefault(4, []).append(("qe", 2, 0, 4))
         for q in range(3, 8):
             v_after.setdefault(4 * q - 4, []).append(("qe", q, 0, 4))
         for n, w, h in ((11, 2, 1), (19, 1, 1), (27, 0, 0), (31, 0, 1)):

@@ -21,9 +21,9 @@ F = 1024
 H = 512
 SPLIT = ((256, 256, 0), (256, 256, 0))
 FS = 256
-XR0 = 4
+XR0 = 2
 XR1 = 12
-XA, XB, XR2 = 1, 3, 20
+XA, XB, XR2 = 0, 3, 20
 MANUAL = True
 SINGLE = 30
 ST2 = 3
@@ -302,11 +302,12 @@ def tile_gnnlayer_pa_kernel(tc, x, e_enc, W_pre, b_pre, out_0, out_1):
 
             return {"mean_t": mean_t, "mean_vg": mean_vg, "mean_sq": mean_sq, "var": var, "std": std, "base_to_psum": base_to_psum, "add_base": add_base, "casts": casts}
 
+        load_w(2, 0, 0)
         nc.sync.dma_start(out=x_sb[:], in_=x_rows)
         load_e(0)
-        for w in (2, 1):
-            for g in range(2):
-                load_w(w, g, 0)
+        load_w(2, 1, 0)
+        load_w(1, 0, 0)
+        load_w(1, 1, 0)
         load_e(1)
         load_e(2)
 
@@ -316,6 +317,9 @@ def tile_gnnlayer_pa_kernel(tc, x, e_enc, W_pre, b_pre, out_0, out_1):
         for g in range(2):
             for u in range(2):
                 nc.tensor.transpose(xt[:, 2 * g + u, :], xwords[:, 256 * g + u : 256 * (g + 1) : 2], ident[:])
+        interleave_w(2, 0, 0, "v", 0, FS)
+        interleave_w(2, 0, 0, "s", FS, H)
+        quant_w(2, 0, 0, 1)
         nc.scalar.copy(
             out=xg[:].bitcast(F32).rearrange("p (g r u) -> p g r u", g=2, u=2),
             in_=xt[:].rearrange("p (g u) r -> p g r u", u=2),
@@ -325,10 +329,7 @@ def tile_gnnlayer_pa_kernel(tc, x, e_enc, W_pre, b_pre, out_0, out_1):
         nc.vector.quantize_mx(out=xc[:].bitcast(FP8X4), scales=xs[:], in_=xg[:])
         for n in range(4):
             nc.vector.tensor_copy(out=xs4[:].rearrange("p (c n) -> p c n", n=4)[:, :, n], in_=xs[:])
-        interleave_w(2, 0, 0, "v", 0, FS)
-        interleave_w(2, 0, 0, "s", FS, H)
         quant(0, 0, 2)
-        quant_w(2, 0, 0, 1)
         interleave_w(2, 1, 0, "v", 0, FS)
         interleave_w(2, 1, 0, "s", FS, H)
         quant_w(2, 0, 1, 2)

from contextlib import ExitStack

import concourse.mybir as mybir
from concourse.masks import make_block_diagonal, make_identity

F32 = mybir.dt.float32
BF16 = mybir.dt.bfloat16
I32 = mybir.dt.int32
U8 = mybir.dt.uint8
FP8X4 = mybir.dt.float8_e4m3fn_x4
FP8 = mybir.dt.float8_e4m3fn
ALU = mybir.AluOpType
ACT = mybir.ActivationFunctionType

FLOPS = 2 * (4096 + 256) * 1024 * 1024

P = 128
NJ = 32
NPR = 16
F = 1024
H = 512
SPLIT = ((256, 256, 0), (256, 256, 0))
FS = 256
XR0 = 2
XR1 = 12
XA, XB, XR2 = 0, 3, 20
MANUAL = True
SINGLE = 30
ST2 = 3
Y_SCALE = 160.0
EPS_STD = 1e-5
INV = 1.0 / 32.0


def tile_gnnlayer_pa_kernel(tc, x, e_enc, W_pre, b_pre, out_0, out_1):
    nc = tc.nc
    x_rows = x.flatten_outer_dims()
    e_rows = e_enc.rearrange("b i j k -> (b i) j k")
    o0 = out_0.flatten_outer_dims().rearrange("p (s f) -> p s f", s=4)
    o1 = out_1.flatten_outer_dims().rearrange("p (s f) -> p s f", s=4)
    sig_off = (0, SPLIT[0][0])
    sig_w = SPLIT[0][0] + SPLIT[1][0]

    with ExitStack() as ctx:
        const = ctx.enter_context(tc.tile_pool(name="const", bufs=1))
        wraw_pool = ctx.enter_context(tc.tile_pool(name="wraw", bufs=4))
        wgrp_pool = ctx.enter_context(tc.tile_pool(name="wgrp", bufs=2))
        eraw_pool = ctx.enter_context(tc.tile_pool(name="eraw", bufs=3))
        egrp_pool = ctx.enter_context(tc.tile_pool(name="egrp", bufs=2))
        st2_pool = ctx.enter_context(tc.tile_pool(name="st2", bufs=ST2))
        shr = ctx.enter_context(tc.tile_pool(name="shr", bufs=1))
        ptp = ctx.enter_context(tc.psum_pool(name="ptp", bufs=1))
        pz = ctx.enter_context(tc.psum_pool(name="pz", bufs=5))
        psig = ctx.enter_context(tc.psum_pool(name="psig", bufs=1))

        warm = const.tile([P, 2], F32, name="warm")
        nc.vector.memset(warm[:, 0:1], 1.0)
        nc.scalar.activation(out=warm[:, 1:2], in_=warm[:, 0:1], func=ACT.Sqrt)
        ident = const.tile([P, P], F32, name="ident")
        make_identity(nc, ident[:])
        bd = const.tile([P, P], F32, name="bd")
        make_block_diagonal(nc, bd[:], 32)
        if MANUAL:
            ctx.enter_context(tc.manual_schedule())

        x_sb = shr.tile([P, 1024], BF16, name="x_sb", tag="shc", align_bytes=64)
        xg = shr.tile([P, 1024], BF16, name="xg", tag="shd", align_bytes=64)
        xc = const.tile([P, 256], I32, name="xc", align_bytes=64)
        xs = const.tile([P, 256], U8, name="xs", align_bytes=64)
        xs4 = const.tile([P, 1024], U8, name="xs4", align_bytes=64)
        xrep_c = const.tile([P, NJ, 2, P], I32, name="xrep_c", align_bytes=64)
        xrep_s = const.tile([P, NJ, 2, P], U8, name="xrep_s", align_bytes=64)
        wc = const.tile([P, 3, 2, 2, H], I32, name="wc", align_bytes=64)
        ws = const.tile([P, 3, 2, 2, H], U8, name="ws", align_bytes=64)
        ec = const.tile([P, NJ, 256], I32, name="ec", align_bytes=64)
        es = const.tile([P, NJ, 256], U8, name="es", align_bytes=64)
        b_bc = const.tile([P, F], BF16, name="b_bc")
        late = {}
        res = [const.tile([P, 4, H], F32, name="res%d" % h) for h in range(2)]
        acc_g = [const.tile([P, 1 + h, H + SPLIT[h][2]], F32, name="acc_g%d" % h) for h in range(2)]
        acc_v = [const.tile([P, SPLIT[h][1]], F32, name="acc_v%d" % h) for h in range(2)]
        o8 = [const.tile([P, 4, H], FP8, name="o8%d" % h) for h in range(2)]
        sig = {0: psig.tile([P, H], F32, name="sig")}

        wraw = {}
        eraw = {}

        def load_w(w, g, h):
            t = wraw_pool.tile([P, 4, H], BF16, name="wraw", tag="wraw")
            r0 = w * 1024 + g * 512
            nc.sync.dma_start(out=t[:], in_=W_pre[r0 : r0 + 512, H * h : H * (h + 1)].rearrange("(p t) f -> p t f", t=4))
            wraw[(w, g, h)] = t

        def load_e(pr):
            t = eraw_pool.tile([P, 2, 1024], BF16, name="eraw", tag="eraw")
            nc.sync.dma_start(out=t[:], in_=e_rows[:, 2 * pr : 2 * pr + 2, :])
            eraw[pr] = t

        def replicate_x(j0, j1):
            nc.vector.tensor_copy(
                out=xrep_c[:, j0:j1, :, :].rearrange("p j g (b i) -> p j (g b) i", b=4),
                in_=xc[:].rearrange("p (c j) -> p j c", c=8)[:, j0:j1, :].unsqueeze(3).to_broadcast([P, j1 - j0, 8, 32]),
            )
            nc.vector.tensor_copy(
                out=xrep_s[:, j0:j1, :, :].rearrange("p j g r -> p j (g r)").bitcast(I32).rearrange("p j (c r) -> p j c r", c=8),
                in_=xs4[:].bitcast(I32).rearrange("p (c j) -> p j c", c=8)[:, j0:j1, :].unsqueeze(3).to_broadcast([P, j1 - j0, 8, 8]),
            )

        wgrp = {}

        def interleave_w(w, g, h, eng, f0=0, f1=H):
            if (w, h) not in wgrp:
                wgrp[(w, h)] = wgrp_pool.tile([P, 2, 2048], BF16, name="wgrp", tag="wgrp", align_bytes=64)
            dst = wgrp[(w, h)][:, g, 4 * f0 : 4 * f1].rearrange("p (c i t) -> p c t i", i=4, t=4)
            src = wraw[(w, g, h)][:, :, f0:f1].rearrange("p t (c i) -> p c t i", i=4)
            if eng == "v":
                nc.vector.tensor_copy(out=dst, in_=src)
            elif eng == "s":
                nc.scalar.copy(out=dst, in_=src)
            else:
                nc.gpsimd.tensor_scalar(out=dst, in0=src, scalar1=1.0, scalar2=0.0, op0=ALU.mult, op1=ALU.add)

        def quant_w(w, h, g0, g1):
            nc.vector.quantize_mx(
                out=wc[:, w, h, g0:g1, :].rearrange("p g f -> p (g f)").bitcast(FP8X4),
                scales=ws[:, w, h, g0:g1, :].rearrange("p g f -> p (g f)"),
                in_=wgrp[(w, h)][:, g0:g1, :].rearrange("p g c -> p (g c)"),
            )

        tps = {}
        egrp = {}

        def transposes(pr, head=False):
            raw = eraw[pr]
            for jj in range(2):
                if head:
                    tp = pz.tile([P, 4, P], F32, name="z", tag="z")
                else:
                    tp = ptp.tile([P, 4, P], F32, name="tp%d" % jj, tag="tp%d" % jj)
                words = raw[:, jj, :].bitcast(F32)
                for g in range(2):
                    for u in range(2):
                        nc.tensor.transpose(tp[:, 2 * g + u, :], words[:, 256 * g + u : 256 * (g + 1) : 2], ident[:])
                tps[(pr, jj)] = tp

        def copy_out(pr):
            q = pr // 2
            if q not in egrp:
                egrp[q] = egrp_pool.tile([P, 4096], BF16, name="egrp", tag="egrp", align_bytes=64)
            gw = egrp[q][:].bitcast(F32).rearrange("p (n g r u) -> p n g r u", n=4, g=2, u=2)
            for jj in range(2):
                nc.scalar.copy(out=gw[:, 2 * (pr % 2) + jj], in_=tps[(pr, jj)][:].rearrange("p (g u) r -> p g r u", u=2))

        def quant(q, n0, n1):
            nc.vector.quantize_mx(
                out=ec[:, 4 * q + n0 : 4 * q + n1, :].rearrange("p j c -> p (j c)").bitcast(FP8X4),
                scales=es[:, 4 * q + n0 : 4 * q + n1, :].rearrange("p j c -> p (j c)"),
                in_=egrp[q][:, 1024 * n0 : 1024 * n1],
            )

        def mx(out, lc, ls, w, h, g, n, start, stop):
            nc.tensor.matmul_mx(
                out=out,
                lhsT=lc.bitcast(FP8X4),
                lhsT_scale=ls,
                rhs=wc[:, w, h, g, 0:n].bitcast(FP8X4),
                rhs_scale=ws[:, w, h, g, 0:n],
                start=start,
                stop=stop,
            )

        def bank(j, h, before_vector=None):
            a_t, b_v, c_g = SPLIT[h]
            hs = slice(H * h, H * (h + 1))
            if h == 1 and j % 7 == 6:
                z = psig.tile([P, H], F32, name="sig")
            elif h == 1 and j % 7 == 5:
                z = ptp.tile([P, H], F32, name="tp1", tag="tp1")
            else:
                z = pz.tile([P, H], F32, name="z", tag="z")

            def sum_passes():
                for g in range(2):
                    mx(sig[h][:, 0:a_t], ec[:, j, 128 * g : 128 * (g + 1)], es[:, j, 128 * g : 128 * (g + 1)], 2, h, g, a_t, j == 0 and g == 0, j == NJ - 1 and g == 1)

            if j == NJ - 1:
                sum_passes()
            for g in range(2):
                mx(z[:], ec[:, j, 128 * g : 128 * (g + 1)], es[:, j, 128 * g : 128 * (g + 1)], 2, h, g, H, g == 0, False)
            for g in range(2):
                mx(z[:], xrep_c[:, j, g, :], xrep_s[:, j, g, :], 1, h, g, H, False, g == 1)
            if j < NJ - 1:
                sum_passes()
            if j <= h:
                dst = acc_g[h][:, j, :]
            else:
                if j % 2 == 0 or j == 1:
                    late["st2"] = st2_pool.tile([P, 2, H + c_g], F32, name="st2", tag="st2")
                dst = late["st2"][:, j % 2, :]
            nc.scalar.activation(out=dst[:, 0:H], in_=z[:], func=ACT.Square)
            if c_g:
                nc.scalar.copy(out=dst[:, H : H + c_g], in_=z[:, H - c_g : H])
            if j == 0:
                nc.scalar.copy(out=res[h][:, 1, :], in_=z[:])
            else:
                if before_vector:
                    before_vector()
                if j == 1:
                    nc.vector.tensor_tensor(out=acc_v[h][:], in0=z[:, a_t : a_t + b_v], in1=res[h][:, 1, a_t : a_t + b_v], op=ALU.add)
                nc.vector.tensor_tensor(out=res[h][:, 2, :], in0=z[:], in1=res[h][:, 1 if j == 1 else 2, :], op=ALU.max)
                nc.vector.tensor_tensor(out=res[h][:, 1, :], in0=z[:], in1=res[h][:, 1, :], op=ALU.min)
                if j > 1:
                    nc.vector.tensor_tensor(out=acc_v[h][:], in0=z[:, a_t : a_t + b_v], in1=acc_v[h][:], op=ALU.add)
                if h == 0:
                    nc.gpsimd.tensor_tensor(out=acc_g[0][:, 0, :], in0=acc_g[0][:, 0, :], in1=dst, op=ALU.add)
                elif j >= SINGLE:
                    add = nc.vector.tensor_tensor if j == NJ - 1 else nc.gpsimd.tensor_tensor
                    add(out=acc_g[1][:, 0, :], in0=acc_g[1][:, 0, :], in1=dst, op=ALU.add)
                elif j % 2 == 1 and j > 1:
                    nc.gpsimd.tensor_tensor(out=acc_g[1][:], in0=acc_g[1][:], in1=late["st2"][:], op=ALU.add)
                    if j == SINGLE - 1:
                        nc.gpsimd.tensor_tensor(out=acc_g[1][:, 0, :], in0=acc_g[1][:, 0, :], in1=acc_g[1][:, 1, :], op=ALU.add)

        def source_sum_a():
            late["s_sb"] = shr.tile([P, sig_w], F32, name="s_sb", tag="shc", align_bytes=64)
            late["srep32"] = shr.tile([P, sig_w], F32, name="srep32", tag="shd", align_bytes=64)
            s_ps = pz.tile([P, H], F32, name="z", tag="z")
            for h in range(2):
                for g in range(2):
                    mx(s_ps[:, sig_off[h] : sig_off[h] + SPLIT[h][0]], xc[:, 128 * g : 128 * (g + 1)], xs[:, 128 * g : 128 * (g + 1)], 1, h, g, SPLIT[h][0], g == 0, g == 1)
            nc.scalar.copy(out=late["s_sb"][:], in_=s_ps[:, 0:sig_w])

        def source_sum_b():
            srep_ps = pz.tile([P, H], F32, name="z", tag="z")
            nc.tensor.matmul(out=srep_ps[:, 0:sig_w], lhsT=bd[:], rhs=late["s_sb"][:], start=True, stop=True)
            nc.scalar.activation(out=late["srep32"][:], in_=srep_ps[:, 0:sig_w], func=ACT.Copy, scale=INV)

        def target_term(h):
            if "base" not in late:
                late["base"] = shr.tile([P, F], F32, name="base", tag="shb", align_bytes=64)
            tg = pz.tile([P, H], F32, name="z", tag="z")
            for g in range(2):
                mx(tg[:], xc[:, 128 * g : 128 * (g + 1)], xs[:, 128 * g : 128 * (g + 1)], 0, h, g, H, g == 0, g == 1)
            nc.vector.tensor_tensor(out=late["base"][:, H * h : H * (h + 1)], in0=tg[:], in1=b_bc[:, H * h : H * (h + 1)], op=ALU.add)

        def cast(eng, s, h):
            if eng == "s":
                nc.scalar.activation(out=o8[h][:, s, :], in_=res[h][:, s, :], func=ACT.Copy, scale=Y_SCALE, saturate=False)
            else:
                nc.vector.tensor_scalar(out=o8[h][:, s, :], in0=res[h][:, s, :], scalar1=Y_SCALE, scalar2=None, op0=ALU.mult, saturate=False)

        def finish_steps(h):
            a_t, b_v, c_g = SPLIT[h]
            d = late["mm"][:, 0, :]
            q = late["mm"][:, 1, :]
            c0 = H * h
            hs = slice(c0, c0 + H)

            def mean_t():
                nc.vector.scalar_tensor_tensor(
                    out=res[h][:, 0, 0:a_t], in0=sig[h][:, 0:a_t], scalar=INV, in1=late["srep32"][:, sig_off[h] : sig_off[h] + a_t], op0=ALU.mult, op1=ALU.add
                )

            def mean_vg():
                nc.scalar.activation(out=res[h][:, 0, a_t : a_t + b_v], in_=acc_v[h][:], func=ACT.Copy, scale=INV)
                if c_g:
                    nc.scalar.activation(out=res[h][:, 0, H - c_g : H], in_=acc_g[h][:, 0, H : H + c_g], func=ACT.Copy, scale=INV)

            def mean_sq():
                nc.scalar.activation(out=d[:, hs], in_=res[h][:, 0, :], func=ACT.Square)
                if h == 0:
                    nc.scalar.activation(out=q[:, hs], in_=acc_g[h][:, 0, 0:H], func=ACT.Copy, scale=INV)

            def var():
                if h == 0:
                    nc.gpsimd.tensor_tensor(out=d[:, hs], in0=q[:, hs], in1=d[:, hs], op=ALU.subtract)
                    nc.gpsimd.tensor_scalar(out=d[:, hs], in0=d[:, hs], scalar1=0.0, scalar2=EPS_STD, op0=ALU.max, op1=ALU.add)
                else:
                    nc.vector.scalar_tensor_tensor(out=d[:, hs], in0=acc_g[h][:, 0, 0:H], scalar=INV, in1=d[:, hs], op0=ALU.mult, op1=ALU.subtract)
                    nc.vector.tensor_scalar(out=d[:, hs], in0=d[:, hs], scalar1=0.0, scalar2=EPS_STD, op0=ALU.max, op1=ALU.add)

            def std():
                nc.scalar.activation(out=res[h][:, 3, :], in_=d[:, hs], func=ACT.Sqrt)
                nc.sync.dma_start(out=o0[:, 3, hs], in_=res[h][:, 3, :])
                cast("s", 3, h)
                nc.sync.dma_start(out=o1[:, 3, hs], in_=o8[h][:, 3, :].bitcast(U8))

            def base_to_psum():
                bp = pz.tile([P, H], F32, name="z", tag="z")
                nc.tensor.matmul(out=bp[:], lhsT=ident[:], rhs=late["base"][:, hs], start=True, stop=True)
                late["bp"] = bp

            def add_base(s0, s1):
                b_in = late["bp"][:] if h == 0 else late["base"][:, hs]
                nc.vector.tensor_tensor(out=res[h][:, s0:s1, :], in0=b_in.unsqueeze(1).to_broadcast([P, s1 - s0, H]), in1=res[h][:, s0:s1, :], op=ALU.add)
                nc.sync.dma_start(out=o0[:, s0:s1, hs], in_=res[h][:, s0:s1, :])

            def casts(s0, s1, engs):
                for s in range(s0, s1):
                    cast(engs[s - s0], s, h)
                nc.sync.dma_start(out=o1[:, s0:s1, hs], in_=o8[h][:, s0:s1, :].bitcast(U8))

            return {"mean_t": mean_t, "mean_vg": mean_vg, "mean_sq": mean_sq, "var": var, "std": std, "base_to_psum": base_to_psum, "add_base": add_base, "casts": casts}

        load_w(2, 0, 0)
        nc.sync.dma_start(out=x_sb[:], in_=x_rows)
        load_e(0)
        load_w(2, 1, 0)
        load_w(1, 0, 0)
        load_w(1, 1, 0)
        load_e(1)
        load_e(2)

        nc.vector.memset(xs[:].bitcast(I32), 0)
        xt = ptp.tile([P, 4, P], F32, name="tp1", tag="tp1")
        xwords = x_sb[:].bitcast(F32)
        for g in range(2):
            for u in range(2):
                nc.tensor.transpose(xt[:, 2 * g + u, :], xwords[:, 256 * g + u : 256 * (g + 1) : 2], ident[:])
        interleave_w(2, 0, 0, "v", 0, FS)
        interleave_w(2, 0, 0, "s", FS, H)
        quant_w(2, 0, 0, 1)
        nc.scalar.copy(
            out=xg[:].bitcast(F32).rearrange("p (g r u) -> p g r u", g=2, u=2),
            in_=xt[:].rearrange("p (g u) r -> p g r u", u=2),
        )
        transposes(0, head=True)
        copy_out(0)
        nc.vector.quantize_mx(out=xc[:].bitcast(FP8X4), scales=xs[:], in_=xg[:])
        for n in range(4):
            nc.vector.tensor_copy(out=xs4[:].rearrange("p (c n) -> p c n", n=4)[:, :, n], in_=xs[:])
        quant(0, 0, 2)
        interleave_w(2, 1, 0, "v", 0, FS)
        interleave_w(2, 1, 0, "s", FS, H)
        quant_w(2, 0, 1, 2)
        replicate_x(0, XR0)
        interleave_w(1, 0, 0, "v", 0, FS)
        interleave_w(1, 0, 0, "s", FS, H)
        quant_w(1, 0, 0, 1)
        interleave_w(1, 1, 0, "v", 0, FS)
        interleave_w(1, 1, 0, "s", FS, H)
        quant_w(1, 0, 1, 2)
        transposes(1, head=True)
        copy_out(1)
        quant(0, 2, 4)
        replicate_x(XR0, XR1)
        load_e(3)
        load_e(4)
        load_w(2, 0, 1)
        load_w(2, 1, 1)

        w_later = [(2, 0, 1), (2, 1, 1), (1, 0, 1), (1, 1, 1), (0, 0, 0), (0, 1, 0), (0, 0, 1), (0, 1, 1)]
        g_pieces = {}
        s_late = {27: 12, 28: 13, 29: 14, 30: 15}
        tr_after = {0: 2, 1: 3, 2: 4, 3: 5}
        for n in range(5, NJ, 2):
            if (n + 7) // 2 < NPR:
                tr_after[n] = (n + 7) // 2
        loads_after = {0: [("e", 5)], 1: [("e", 6), ("w", 1, 0, 1), ("w", 1, 1, 1)], 2: [("e", 7)], 3: [("e", 8)], 7: [("w", 0, 0, 0)], 11: [("w", 0, 1, 0)], 15: [("w", 0, 0, 1)], 19: [("w", 0, 1, 1)]}
        for n in range(5, NJ, 2):
            if (n + 7) // 2 + 3 < NPR:
                loads_after.setdefault(n, []).append(("e", (n + 7) // 2 + 3))
        v_after = {XA: [("xr", XR1, XR2)]}
        v_after.setdefault(XB, []).append(("xr", XR2, NJ))
        v_after.setdefault(2, []).append(("qe", 1, 0, 4))
        v_after.setdefault(4, []).append(("qe", 2, 0, 4))
        for q in range(3, 8):
            v_after.setdefault(4 * q - 4, []).append(("qe", q, 0, 4))
        for n, w, h in ((11, 2, 1), (19, 1, 1), (27, 0, 0), (31, 0, 1)):
            v_after.setdefault(n, []).append(("qw", w, h))

        def il_piece(n, eng="s"):
            w, g, h = w_later[n // 2]
            interleave_w(w, g, h, eng, 256 * (n % 2), 256 * (n % 2 + 1))

        late["mm"] = shr.tile([P, 2, F], F32, name="mm", tag="sha", align_bytes=64)
        f0 = finish_steps(0)
        for j in range(NJ):
            bank(j, 0, f0["mean_t"] if j == NJ - 1 else None)
            if j % 2 == 0 and 4 <= j <= 26:
                il_piece(j // 2 - 2)
            if j in s_late:
                il_piece(s_late[j])
            for a in v_after.get(j, []):
                if a[0] == "qe":
                    quant(a[1], a[2], a[3])
                elif a[0] == "xr":
                    replicate_x(a[1], a[2])
                else:
                    quant_w(a[1], a[2], 0, 2)
            if j in tr_after:
                transposes(tr_after[j])
                copy_out(tr_after[j])
            for a in loads_after.get(j, []):
                if a[0] == "e":
                    load_e(a[1])
                else:
                    load_w(a[1], a[2], a[3])
            if j == 4:
                nc.sync.dma_start(out=b_bc[:], in_=b_pre.partition_broadcast(P))
            if j == 22:
                source_sum_a()
            if j == 24:
                source_sum_b()

        sig[1] = ptp.tile([P, H], F32, name="tp0", tag="tp0")
        f1 = finish_steps(1)
        for j in range(NJ):
            bank(j, 1, f1["mean_t"] if j == NJ - 1 else None)
            if j in (2, 3):
                target_term(0 if j == 2 else 1)
            if j == 0:
                f0["mean_vg"]()
            if j == 1:
                f0["mean_sq"]()
            if j == 1:
                f0["var"]()
            if j == 5:
                f0["base_to_psum"]()
            if j == 7:
                f0["add_base"](0, 3)
            if j == 9:
                f0["std"]()
            if j == 11:
                f0["casts"](0, 3, "sss")
        f1["mean_vg"]()
        f1["mean_sq"]()
        f1["add_base"](1, 3)
        f1["var"]()
        f1["casts"](1, 3, "ss")
        f1["std"]()
        f1["add_base"](0, 1)
        f1["casts"](0, 1, "v")
